import numpy as np
import ml_dtypes


def mxq(x, axis, fmt="e4m3"):
    dtype, down = {"e4m3": (ml_dtypes.float8_e4m3fn, 7), "e5m2": (ml_dtypes.float8_e5m2, 14)}[fmt]
    v = np.moveaxis(np.asarray(x, np.float32).astype(ml_dtypes.bfloat16).astype(np.float64), axis, -1)
    blocks = v.reshape(v.shape[:-1] + (-1, 32))
    amax = np.abs(blocks).max(-1, keepdims=True)
    byte = np.maximum(np.where(amax > 0, np.frexp(amax)[1] - 1 + 127, 0) - down, 1)
    scale = np.exp2(byte - 127.0)
    codes = (blocks / scale).astype(np.float32).astype(dtype).astype(np.float64)
    return np.moveaxis((codes * scale).reshape(v.shape), -1, axis)


WIDE = False


def mx_kscale(k):
    if not WIDE:
        return np.ones(k)
    levels = np.array([10, -10, 5, -5, 0])
    a = np.random.permutation(np.resize(levels, k // 512 * 4)).reshape(k // 512, 4)
    idx = np.arange(k)
    return np.exp2(a[idx // 512, idx % 128 // 32])


BF16 = ml_dtypes.bfloat16


def bf(x):
    return np.asarray(x, np.float32).astype(BF16)


def f64(x):
    return np.asarray(x).astype(np.float64)


E2M1 = np.array([0.0, 0.5, 1.0, 1.5, 2.0, 3.0, 4.0, 6.0, -0.0, -0.5, -1.0, -1.5, -2.0, -3.0, -4.0, -6.0])


def pack_weight(w, fmt):
    k, n = w.shape
    w = f64(bf(w)).reshape(k // 32, 32, n)
    amax = np.abs(w).max(1)
    if fmt == "e4m3":
        byte = np.frexp(amax)[1] - 1 + 127 - 7
    else:
        mant, ex = np.frexp(amax / 6.0)
        byte = np.where(mant > 0.5, ex, ex - 1) + 127
    byte = np.clip(np.where(amax > 0, byte, 1), 1, 254)
    scaled = (w * np.exp2(127.0 - byte)[:, None, :]).reshape(k, n).astype(np.float32)
    by_word = np.ascontiguousarray(scaled.reshape(k // 512, 128, 4, n).transpose(0, 1, 3, 2))
    if fmt == "e4m3":
        words = by_word.astype(ml_dtypes.float8_e4m3fn).view(np.uint8)
    else:
        c = by_word.astype(ml_dtypes.float4_e2m1fn).view(np.uint8) & 0xF
        words = c[..., 0::2] | (c[..., 1::2] << 4)
    return np.ascontiguousarray(words), np.ascontiguousarray(byte.astype(np.uint8).reshape(k // 512, 16, n))


def unpack_weight(words, scales, fmt):
    g, p, n, _ = words.shape
    if fmt == "e4m3":
        vals = np.ascontiguousarray(words).view(ml_dtypes.float8_e4m3fn).astype(np.float64)
    else:
        nib = np.empty((g, p, n, 4), np.uint8)
        nib[..., 0::2] = words & 0xF
        nib[..., 1::2] = words >> 4
        vals = E2M1[nib]
    vals = vals * np.repeat(np.exp2(scales.astype(np.float64) - 127.0), 8, axis=1)[..., None]
    return vals.transpose(0, 1, 3, 2).reshape(g * 512, n)


B, C, H, W, S, HID, OC = 2, 128, 64, 64, 2, 1024, 256
H2, W2 = H // S, W // S
K1 = C * S * S
RESIDUAL = True
FMT = "e4m3"


def setup_inputs():
    s = mx_kscale(K1)
    s = s / s.max()
    sx = np.broadcast_to(s.reshape(C, 1, S, 1, S), (C, H2, S, W2, S)).reshape(C, H, W)
    x = bf(np.random.standard_normal((B, C, H, W)) * sx)
    w1 = np.random.standard_normal((HID, K1)) / np.sqrt(K1) / s
    weight1_words, weight1_scales = pack_weight(np.ascontiguousarray(w1.T), FMT)
    bias1 = bf(np.random.standard_normal(HID) * 0.2)
    w2 = np.random.standard_normal((OC, HID)) * 1.5 / np.sqrt(HID)
    weight2_words, weight2_scales = pack_weight(np.ascontiguousarray(w2.T), FMT)
    bias2 = bf(np.random.standard_normal(OC) * 0.2)
    return {"x": x,
            "weight1_words": weight1_words,
            "weight1_scales": weight1_scales,
            "bias1": bias1,
            "weight2_words": weight2_words,
            "weight2_scales": weight2_scales,
            "bias2": bias2}


def reference(x, weight1_words, weight1_scales, bias1, weight2_words, weight2_scales, bias2):
    x = f64(x)
    p = x.reshape(B, C, H2, S, W2, S)
    p = p.transpose(0, 2, 4, 1, 3, 5).reshape(B * H2 * W2, C * S * S)
    o1 = (mxq(p, 1, "e4m3") @ unpack_weight(weight1_words, weight1_scales, FMT)) + f64(bias1)
    o2 = o1 * (1.0 / (1.0 + np.exp(-o1)))
    o3 = (mxq(o2, 1, "e4m3") @ unpack_weight(weight2_words, weight2_scales, FMT)) + f64(bias2)
    out = o3.reshape(B, H2, W2, -1).transpose(0, 3, 1, 2)
    if RESIDUAL:
        pooled = x.reshape(B, C, H2, S, W2, S).mean(axis=(3, 5))
        n = out.shape[1] // C
        res = np.repeat(pooled, n, axis=1)
        out = out + res
    return out

@@ -1,0 +1,273 @@
+from contextlib import ExitStack
+
+import concourse.mybir as mybir
+from concourse.masks import make_identity
+
+F32 = mybir.dt.float32
+BF16 = mybir.dt.bfloat16
+I32 = mybir.dt.int32
+U32 = mybir.dt.uint32
+U8 = mybir.dt.uint8
+FP8X4 = mybir.dt.float8_e4m3fn_x4
+ADD = mybir.AluOpType.add
+SILU = mybir.ActivationFunctionType.Silu
+IDENTITY = mybir.ActivationFunctionType.Identity
+
+P = 128
+PACK = 4
+K_PASS = P * PACK
+BANK = 512
+
+BATCH, CHANNELS, HEIGHT, WIDTH = 2, 128, 64, 64
+HIDDEN, OUT_CHANNELS = 1024, 256
+TOKENS = BATCH * (HEIGHT // 2) * (WIDTH // 2)
+TOKENS_PER_IMAGE = TOKENS // BATCH
+
+ROUND = BANK
+ROUNDS = TOKENS // ROUND
+ROUNDS_PER_IMAGE = ROUNDS // BATCH
+TILES_PER_ROUND = ROUND // P
+TOKEN_TILES = TOKENS // P
+PATCH_ROWS = ROUND // (WIDTH // 2)
+HIDDEN_PASSES = HIDDEN // K_PASS
+OUT_TILES = OUT_CHANNELS // P
+
+FLOPS = 2 * TOKENS * (CHANNELS * PACK) * HIDDEN + 2 * TOKENS * HIDDEN * OUT_CHANNELS
+
+
+def tile_memoryefficientpatchdownscale_kernel(
+    tc, x, weight1_words, weight1_scales, bias1, weight2_words, weight2_scales, bias2, out
+):
+    nc = tc.nc
+    with ExitStack() as ctx:
+        keep = ctx.enter_context(tc.tile_pool(name="keep", bufs=1))
+        work = ctx.enter_context(tc.tile_pool(name="work", bufs=2))
+        psum_stream = ctx.enter_context(tc.psum_pool(name="psum_stream", bufs=3))
+        psum_out = ctx.enter_context(tc.psum_pool(name="psum_out", bufs=2))
+
+        w1_scales = keep.tile([P, HIDDEN], U8, align_bytes=64)
+        w2_scales = keep.tile([P, HIDDEN_PASSES, OUT_CHANNELS], U8, align_bytes=64)
+        nc.vector.memset(w1_scales[:].bitcast(I32), 0)
+        nc.vector.memset(w2_scales[:].rearrange("q g n -> q (g n)").bitcast(I32), 0)
+
+        bias1_row = keep.tile([P, HIDDEN], BF16)
+        ones = keep.tile([P, P], BF16)
+        nc.vector.memset(bias1_row[:], 0.0)
+        nc.vector.memset(ones[:], 1.0)
+        nc.scalar.dma_start(out=bias1_row[0:1, :], in_=bias1.unsqueeze(0))
+
+        table_in = keep.tile([P, 1], F32)
+        table_out = keep.tile([P, 1], F32)
+        nc.vector.memset(table_in[:], 0.0)
+        nc.scalar.activation(out=table_out[:], in_=table_in[:], func=SILU)
+
+        x_rows = keep.tile([P, ROUNDS, PACK * ROUND], BF16)
+        x_pairs = keep.tile([P, OUT_TILES, BATCH, TOKENS_PER_IMAGE * 2], BF16)
+        w1_codes = keep.tile([P, HIDDEN], U32, align_bytes=64)
+        w2_codes = keep.tile([P, HIDDEN_PASSES, OUT_CHANNELS], U32, align_bytes=64)
+        bias2_col = keep.tile([P, OUT_TILES], BF16)
+
+        def load_x_rows(r):
+            b, half = divmod(r, ROUNDS_PER_IMAGE)
+            image = x[b].rearrange("c h w -> c (h w)")
+            nc.sync.dma_start(
+                out=x_rows[:, r, :], in_=image[:, half * PACK * ROUND : (half + 1) * PACK * ROUND]
+            )
+
+        def load_x_pairs(b):
+            for m in range(OUT_TILES):
+                channels = x[b, m * (P // 2) : (m + 1) * (P // 2)].rearrange("c (i u) w -> u c i w", u=2)
+                for u in range(2):
+                    nc.sync.dma_start(
+                        out=x_pairs[u:P:2, m, b, :].rearrange("k (i w) -> k i w", w=WIDTH),
+                        in_=channels[u],
+                    )
+
+        load_x_rows(0)
+        for quadrant in range(4):
+            nc.sync.dma_start(
+                out=w1_scales[32 * quadrant : 32 * quadrant + 4, :].bitcast(I32),
+                in_=weight1_scales[0, 4 * quadrant : 4 * quadrant + 4, :].bitcast(I32),
+            )
+        w1_bytes = weight1_words[0].rearrange("p n t -> p (n t)").bitcast(I32)
+        for g in range(HIDDEN_PASSES):
+            nc.sync.dma_start(
+                out=w1_codes[:, g * BANK : (g + 1) * BANK].bitcast(I32),
+                in_=w1_bytes[:, g * BANK : (g + 1) * BANK],
+            )
+        load_x_rows(1)
+        for quadrant in range(4):
+            nc.sync.dma_start(
+                out=w2_scales[32 * quadrant : 32 * quadrant + 4, :, :].bitcast(I32),
+                in_=weight2_scales[:, 4 * quadrant : 4 * quadrant + 4, :]
+                .rearrange("g r n -> r g n")
+                .bitcast(I32),
+            )
+        for g in range(HIDDEN_PASSES):
+            nc.sync.dma_start(
+                out=w2_codes[:, g, :].bitcast(I32),
+                in_=weight2_words[g].rearrange("p n t -> p (n t)").bitcast(I32),
+            )
+        with nc.allow_non_contiguous_dma(reason="256 bias values, one to a partition"):
+            nc.scalar.dma_start(out=bias2_col[:], in_=bias2.rearrange("(m r) -> r m", r=P))
+        load_x_pairs(0)
+        load_x_rows(2)
+        load_x_rows(3)
+        load_x_pairs(1)
+
+        identity = keep.tile([P, P], F32)
+        make_identity(nc, identity[:])
+
+        identity_pairs = identity[:].rearrange("k (c n) -> k c n", n=2)
+        same_channel = keep.tile([P, P // 2], F32)
+        pool_and_repeat = keep.tile([P, P // 2, 2], BF16)
+        nc.vector.tensor_tensor(
+            out=same_channel[:], in0=identity_pairs[:, :, 0], in1=identity_pairs[:, :, 1], op=ADD
+        )
+        nc.vector.tensor_scalar_mul(
+            out=pool_and_repeat[:],
+            in0=same_channel[:].unsqueeze(2).to_broadcast([P, P // 2, 2]),
+            scalar1=0.25,
+        )
+
+        bias1_sorted = keep.tile([P, HIDDEN_PASSES, PACK, P], F32)
+        for g in range(HIDDEN_PASSES):
+            bias1_rep = psum_out.tile([P, BANK], F32, tag="out_bank")
+            nc.tensor.matmul(
+                out=bias1_rep[:], lhsT=ones[:], rhs=bias1_row[:, g * BANK : (g + 1) * BANK], start=True, stop=True
+            )
+            nc.vector.tensor_copy(
+                out=bias1_sorted[:, g], in_=bias1_rep[:].rearrange("n (q t) -> n t q", t=PACK)
+            )
+
+        p_codes = keep.tile([P, ROUNDS, ROUND], U32, align_bytes=64)
+        p_scales = keep.tile([P, ROUNDS, ROUND], U8, align_bytes=64)
+
+        def quantise_patches(r):
+            patches = work.tile([P, PACK * ROUND], BF16, align_bytes=64)
+            nc.scalar.copy(
+                out=patches[:].bitcast(F32).rearrange("c (i j u) -> c i j u", i=PATCH_ROWS, u=2),
+                in_=x_rows[:, r, :].bitcast(F32).rearrange("c (i u j) -> c i j u", i=PATCH_ROWS, u=2),
+            )
+            nc.vector.quantize_mx(
+                out=p_codes[:, r, :].bitcast(FP8X4), scales=p_scales[:, r, :], in_=patches[:]
+            )
+
+        def first_layer(tile_index):
+            r, k = divmod(tile_index, TILES_PER_ROUND)
+            tokens = slice(k * P, (k + 1) * P)
+            halves = []
+            for g in range(HIDDEN_PASSES):
+                o1 = psum_stream.tile([P, BANK], F32, tag="o1")
+                nc.tensor.matmul_mx(
+                    out=o1[:],
+                    lhsT=p_codes[:, r, tokens].bitcast(FP8X4),
+                    lhsT_scale=p_scales[:, r, tokens],
+                    rhs=w1_codes[:, g * BANK : (g + 1) * BANK].bitcast(FP8X4),
+                    rhs_scale=w1_scales[:, g * BANK : (g + 1) * BANK],
+                    start=True,
+                    stop=True,
+                )
+                o1_sorted = work.tile([P, PACK, P], F32, tag="o1_sorted", bufs=6)
+                nc.vector.tensor_tensor(
+                    out=o1_sorted[:],
+                    in0=o1[:].rearrange("n (q t) -> n t q", t=PACK),
+                    in1=bias1_sorted[:, g],
+                    op=ADD,
+                )
+                halves.append(o1_sorted)
+            return halves
+
+        def activate(tile_index, halves, o2_grouped):
+            k = tile_index % TILES_PER_ROUND
+            for g in range(HIDDEN_PASSES):
+                o1_t = psum_stream.tile([P, PACK, P], F32, tag="o1_t")
+                for t in range(PACK):
+                    nc.tensor.transpose(o1_t[:, t, :], halves[g][:, t, :], identity[:])
+                nc.scalar.activation(
+                    out=o2_grouped[g][:, k * P : (k + 1) * P, :],
+                    in_=o1_t[:].rearrange("q t n -> q n t"),
+                    func=SILU,
+                )
+
+        def residual(r):
+            b, half = divmod(r, ROUNDS_PER_IMAGE)
+            tiles = []
+            for m in range(OUT_TILES):
+                by_v = x_pairs[:, m, b, half * 2 * ROUND : (half + 1) * 2 * ROUND].rearrange(
+                    "k (n v) -> k n v", v=2
+                )
+                pooled = psum_out.tile([P, BANK], F32, tag="out_bank")
+                for v in range(2):
+                    nc.tensor.matmul(
+                        out=pooled[:],
+                        lhsT=pool_and_repeat[:].rearrange("k c n -> k (c n)"),
+                        rhs=by_v[:, :, v],
+                        start=(v == 0),
+                        stop=(v == 1),
+                    )
+                shortcut = work.tile([P, BANK], F32, tag="shortcut", bufs=4)
+                nc.scalar.activation(
+                    out=shortcut[:], in_=pooled[:], func=IDENTITY, bias=bias2_col[:, m : m + 1]
+                )
+                tiles.append(shortcut)
+            return tiles
+
+        def second_layer(r, o2_grouped, shortcuts):
+            b, half = divmod(r, ROUNDS_PER_IMAGE)
+            o2_codes = work.tile([P, HIDDEN_PASSES, ROUND], U32, align_bytes=64)
+            o2_scales = work.tile([P, HIDDEN_PASSES, ROUND], U8, align_bytes=64)
+            for g in range(HIDDEN_PASSES):
+                nc.vector.quantize_mx(
+                    out=o2_codes[:, g, :].bitcast(FP8X4),
+                    scales=o2_scales[:, g, :],
+                    in_=o2_grouped[g][:].rearrange("q n t -> q (n t)"),
+                )
+            sums = []
+            for m in range(OUT_TILES):
+                o3 = psum_out.tile([P, BANK], F32, tag="out_bank")
+                sums.append(o3)
+            for g in range(HIDDEN_PASSES):
+                for m in range(OUT_TILES):
+                    nc.tensor.matmul_mx(
+                        out=sums[m][:],
+                        lhsT=w2_codes[:, g, m * P : (m + 1) * P].bitcast(FP8X4),
+                        lhsT_scale=w2_scales[:, g, m * P : (m + 1) * P],
+                        rhs=o2_codes[:, g, :].bitcast(FP8X4),
+                        rhs_scale=o2_scales[:, g, :],
+                        start=(g == 0),
+                        stop=(g == HIDDEN_PASSES - 1),
+                    )
+            for m in range(OUT_TILES):
+                result = work.tile([P, BANK], F32, tag="result", bufs=4)
+                nc.vector.tensor_tensor(out=result[:], in0=sums[m][:], in1=shortcuts[m][:], op=ADD)
+                nc.sync.dma_start(
+                    out=out[b, m * P : (m + 1) * P].rearrange("o i j -> o (i j)")[
+                        :, half * ROUND : (half + 1) * ROUND
+                    ],
+                    in_=result[:],
+                )
+
+        o2_grouped = {}
+        shortcuts = {}
+        halves = {}
+        quantise_patches(0)
+        for tile_index in range(TOKEN_TILES + 2):
+            r, k = divmod(tile_index, TILES_PER_ROUND)
+            if tile_index < TOKEN_TILES:
+                halves[tile_index] = first_layer(tile_index)
+                if k == 1 and r + 1 < ROUNDS:
+                    quantise_patches(r + 1)
+            if 1 <= tile_index <= TOKEN_TILES:
+                before = tile_index - 1
+                if before % TILES_PER_ROUND == 0:
+                    o2_grouped[before // TILES_PER_ROUND] = [
+                        work.tile([P, ROUND, PACK], BF16, name="o2_grouped_%d" % g, align_bytes=64)
+                        for g in range(HIDDEN_PASSES)
+                    ]
+                activate(before, halves[before], o2_grouped[before // TILES_PER_ROUND])
+                if before % TILES_PER_ROUND == TILES_PER_ROUND - 2:
+                    shortcuts[before // TILES_PER_ROUND] = residual(before // TILES_PER_ROUND)
+            if tile_index >= 2 and (tile_index - 2) % TILES_PER_ROUND == TILES_PER_ROUND - 1:
+                done = (tile_index - 2) // TILES_PER_ROUND
+                second_layer(done, o2_grouped[done], shortcuts[done])

@@ -23,16 +23,33 @@ HIDDEN, OUT_CHANNELS = 1024, 256
 TOKENS = BATCH * (HEIGHT // 2) * (WIDTH // 2)
 TOKENS_PER_IMAGE = TOKENS // BATCH
 
+TOKEN_TILES = TOKENS // P
+TILES_PER_IMAGE = TOKEN_TILES // BATCH
+PATCH_ROWS = P // (WIDTH // 2)
 ROUND = BANK
 ROUNDS = TOKENS // ROUND
 ROUNDS_PER_IMAGE = ROUNDS // BATCH
 TILES_PER_ROUND = ROUND // P
-TOKEN_TILES = TOKENS // P
-PATCH_ROWS = ROUND // (WIDTH // 2)
 HIDDEN_PASSES = HIDDEN // K_PASS
 OUT_TILES = OUT_CHANNELS // P
 
 FLOPS = 2 * TOKENS * (CHANNELS * PACK) * HIDDEN + 2 * TOKENS * HIDDEN * OUT_CHANNELS
+
+REGROUP_AHEAD = 3
+QUANTISE_AHEAD = 2
+ACTIVATE_LAG = 1
+RESIDUAL_LAG = 4
+QUANTISE_O2_LAG = 5
+SECOND_LAYER_LAG = 6
+FINISH_LAG = 7
+SLOTS = TILES_PER_ROUND * (ROUNDS - 1) + FINISH_LAG + 2
+
+
+def part_due(slot, lag):
+    r, part = divmod(slot - lag, TILES_PER_ROUND)
+    if 0 <= r < ROUNDS and part < 2:
+        return r, part
+    return None
 
 
 def tile_memoryefficientpatchdownscale_kernel(
@@ -42,8 +59,8 @@ def tile_memoryefficientpatchdownscale_kernel(
     with ExitStack() as ctx:
         keep = ctx.enter_context(tc.tile_pool(name="keep", bufs=1))
         work = ctx.enter_context(tc.tile_pool(name="work", bufs=2))
-        psum_stream = ctx.enter_context(tc.psum_pool(name="psum_stream", bufs=3))
-        psum_out = ctx.enter_context(tc.psum_pool(name="psum_out", bufs=2))
+        psum = ctx.enter_context(tc.psum_pool(name="psum", bufs=2))
+        ctx.enter_context(tc.manual_schedule())
 
         w1_scales = keep.tile([P, HIDDEN], U8, align_bytes=64)
         w2_scales = keep.tile([P, HIDDEN_PASSES, OUT_CHANNELS], U8, align_bytes=64)
@@ -55,23 +72,25 @@ def tile_memoryefficientpatchdownscale_kernel(
         nc.vector.memset(bias1_row[:], 0.0)
         nc.vector.memset(ones[:], 1.0)
         nc.scalar.dma_start(out=bias1_row[0:1, :], in_=bias1.unsqueeze(0))
+        bias2_col = keep.tile([P, OUT_TILES], BF16)
+        with nc.allow_non_contiguous_dma(reason="256 bias values, one to a partition"):
+            nc.scalar.dma_start(out=bias2_col[:], in_=bias2.rearrange("(m r) -> r m", r=P))
 
         table_in = keep.tile([P, 1], F32)
         table_out = keep.tile([P, 1], F32)
         nc.vector.memset(table_in[:], 0.0)
         nc.scalar.activation(out=table_out[:], in_=table_in[:], func=SILU)
 
-        x_rows = keep.tile([P, ROUNDS, PACK * ROUND], BF16)
+        x_rows = keep.tile([P, TOKEN_TILES, PACK * P], BF16)
         x_pairs = keep.tile([P, OUT_TILES, BATCH, TOKENS_PER_IMAGE * 2], BF16)
         w1_codes = keep.tile([P, HIDDEN], U32, align_bytes=64)
         w2_codes = keep.tile([P, HIDDEN_PASSES, OUT_CHANNELS], U32, align_bytes=64)
-        bias2_col = keep.tile([P, OUT_TILES], BF16)
 
-        def load_x_rows(r):
-            b, half = divmod(r, ROUNDS_PER_IMAGE)
+        def load_x_rows(tile_index):
+            b, k = divmod(tile_index, TILES_PER_IMAGE)
             image = x[b].rearrange("c h w -> c (h w)")
             nc.sync.dma_start(
-                out=x_rows[:, r, :], in_=image[:, half * PACK * ROUND : (half + 1) * PACK * ROUND]
+                out=x_rows[:, tile_index, :], in_=image[:, k * PACK * P : (k + 1) * PACK * P]
             )
 
         def load_x_pairs(b):
@@ -83,36 +102,41 @@ def tile_memoryefficientpatchdownscale_kernel(
                         in_=channels[u],
                     )
 
+        def load_weight1():
+            for quadrant in range(4):
+                nc.sync.dma_start(
+                    out=w1_scales[32 * quadrant : 32 * quadrant + 4, :].bitcast(I32),
+                    in_=weight1_scales[0, 4 * quadrant : 4 * quadrant + 4, :].bitcast(I32),
+                )
+            w1_bytes = weight1_words[0].rearrange("p n t -> p (n t)").bitcast(I32)
+            for g in range(HIDDEN_PASSES):
+                nc.sync.dma_start(
+                    out=w1_codes[:, g * BANK : (g + 1) * BANK].bitcast(I32),
+                    in_=w1_bytes[:, g * BANK : (g + 1) * BANK],
+                )
+
+        def load_weight2():
+            for quadrant in range(4):
+                nc.sync.dma_start(
+                    out=w2_scales[32 * quadrant : 32 * quadrant + 4, :, :].bitcast(I32),
+                    in_=weight2_scales[:, 4 * quadrant : 4 * quadrant + 4, :]
+                    .rearrange("g r n -> r g n")
+                    .bitcast(I32),
+                )
+            for g in range(HIDDEN_PASSES):
+                nc.sync.dma_start(
+                    out=w2_codes[:, g, :].bitcast(I32),
+                    in_=weight2_words[g].rearrange("p n t -> p (n t)").bitcast(I32),
+                )
+
         load_x_rows(0)
-        for quadrant in range(4):
-            nc.sync.dma_start(
-                out=w1_scales[32 * quadrant : 32 * quadrant + 4, :].bitcast(I32),
-                in_=weight1_scales[0, 4 * quadrant : 4 * quadrant + 4, :].bitcast(I32),
-            )
-        w1_bytes = weight1_words[0].rearrange("p n t -> p (n t)").bitcast(I32)
-        for g in range(HIDDEN_PASSES):
-            nc.sync.dma_start(
-                out=w1_codes[:, g * BANK : (g + 1) * BANK].bitcast(I32),
-                in_=w1_bytes[:, g * BANK : (g + 1) * BANK],
-            )
-        load_x_rows(1)
-        for quadrant in range(4):
-            nc.sync.dma_start(
-                out=w2_scales[32 * quadrant : 32 * quadrant + 4, :, :].bitcast(I32),
-                in_=weight2_scales[:, 4 * quadrant : 4 * quadrant + 4, :]
-                .rearrange("g r n -> r g n")
-                .bitcast(I32),
-            )
-        for g in range(HIDDEN_PASSES):
-            nc.sync.dma_start(
-                out=w2_codes[:, g, :].bitcast(I32),
-                in_=weight2_words[g].rearrange("p n t -> p (n t)").bitcast(I32),
-            )
-        with nc.allow_non_contiguous_dma(reason="256 bias values, one to a partition"):
-            nc.scalar.dma_start(out=bias2_col[:], in_=bias2.rearrange("(m r) -> r m", r=P))
+        load_weight1()
+        for tile_index in range(1, TILES_PER_IMAGE):
+            load_x_rows(tile_index)
         load_x_pairs(0)
-        load_x_rows(2)
-        load_x_rows(3)
+        load_weight2()
+        for tile_index in range(TILES_PER_IMAGE, TOKEN_TILES):
+            load_x_rows(tile_index)
         load_x_pairs(1)
 
         identity = keep.tile([P, P], F32)
@@ -130,39 +154,47 @@ def tile_memoryefficientpatchdownscale_kernel(
             scalar1=0.25,
         )
 
+        p_codes = keep.tile([P, TOKEN_TILES, P], U32, align_bytes=64)
+        p_scales = keep.tile([P, TOKEN_TILES, P], U8, align_bytes=64)
         bias1_sorted = keep.tile([P, HIDDEN_PASSES, PACK, P], F32)
-        for g in range(HIDDEN_PASSES):
-            bias1_rep = psum_out.tile([P, BANK], F32, tag="out_bank")
-            nc.tensor.matmul(
-                out=bias1_rep[:], lhsT=ones[:], rhs=bias1_row[:, g * BANK : (g + 1) * BANK], start=True, stop=True
-            )
-            nc.vector.tensor_copy(
-                out=bias1_sorted[:, g], in_=bias1_rep[:].rearrange("n (q t) -> n t q", t=PACK)
-            )
 
-        p_codes = keep.tile([P, ROUNDS, ROUND], U32, align_bytes=64)
-        p_scales = keep.tile([P, ROUNDS, ROUND], U8, align_bytes=64)
-
-        def quantise_patches(r):
-            patches = work.tile([P, PACK * ROUND], BF16, align_bytes=64)
+        def regroup_patches(tile_index):
+            patches = work.tile([P, PACK * P], BF16, tag="patches", bufs=4, align_bytes=64)
             nc.scalar.copy(
                 out=patches[:].bitcast(F32).rearrange("c (i j u) -> c i j u", i=PATCH_ROWS, u=2),
-                in_=x_rows[:, r, :].bitcast(F32).rearrange("c (i u j) -> c i j u", i=PATCH_ROWS, u=2),
+                in_=x_rows[:, tile_index, :].bitcast(F32).rearrange("c (i u j) -> c i j u", i=PATCH_ROWS, u=2),
             )
+            return patches
+
+        def quantise_patches(tile_index, patches):
             nc.vector.quantize_mx(
-                out=p_codes[:, r, :].bitcast(FP8X4), scales=p_scales[:, r, :], in_=patches[:]
+                out=p_codes[:, tile_index, :].bitcast(FP8X4),
+                scales=p_scales[:, tile_index, :],
+                in_=patches[:],
             )
 
+        def spread_bias1():
+            for g in range(HIDDEN_PASSES):
+                bias1_rep = psum.tile([P, BANK], F32, tag="pooled", bufs=1)
+                nc.tensor.matmul(
+                    out=bias1_rep[:],
+                    lhsT=ones[:],
+                    rhs=bias1_row[:, g * BANK : (g + 1) * BANK],
+                    start=True,
+                    stop=True,
+                )
+                nc.scalar.copy(
+                    out=bias1_sorted[:, g], in_=bias1_rep[:].rearrange("n (q t) -> n t q", t=PACK)
+                )
+
         def first_layer(tile_index):
-            r, k = divmod(tile_index, TILES_PER_ROUND)
-            tokens = slice(k * P, (k + 1) * P)
             halves = []
             for g in range(HIDDEN_PASSES):
-                o1 = psum_stream.tile([P, BANK], F32, tag="o1")
+                o1 = psum.tile([P, BANK], F32, tag="o1", bufs=2)
                 nc.tensor.matmul_mx(
                     out=o1[:],
-                    lhsT=p_codes[:, r, tokens].bitcast(FP8X4),
-                    lhsT_scale=p_scales[:, r, tokens],
+                    lhsT=p_codes[:, tile_index, :].bitcast(FP8X4),
+                    lhsT_scale=p_scales[:, tile_index, :],
                     rhs=w1_codes[:, g * BANK : (g + 1) * BANK].bitcast(FP8X4),
                     rhs_scale=w1_scales[:, g * BANK : (g + 1) * BANK],
                     start=True,
@@ -181,7 +213,7 @@ def tile_memoryefficientpatchdownscale_kernel(
         def activate(tile_index, halves, o2_grouped):
             k = tile_index % TILES_PER_ROUND
             for g in range(HIDDEN_PASSES):
-                o1_t = psum_stream.tile([P, PACK, P], F32, tag="o1_t")
+                o1_t = psum.tile([P, PACK, P], F32, tag="o1_t", bufs=3)
                 for t in range(PACK):
                     nc.tensor.transpose(o1_t[:, t, :], halves[g][:, t, :], identity[:])
                 nc.scalar.activation(
@@ -190,84 +222,106 @@ def tile_memoryefficientpatchdownscale_kernel(
                     func=SILU,
                 )
 
-        def residual(r):
+        def residual(r, m):
             b, half = divmod(r, ROUNDS_PER_IMAGE)
-            tiles = []
-            for m in range(OUT_TILES):
-                by_v = x_pairs[:, m, b, half * 2 * ROUND : (half + 1) * 2 * ROUND].rearrange(
-                    "k (n v) -> k n v", v=2
+            by_v = x_pairs[:, m, b, half * 2 * ROUND : (half + 1) * 2 * ROUND].rearrange(
+                "k (n v) -> k n v", v=2
+            )
+            pooled = psum.tile([P, BANK], F32, tag="pooled", bufs=1)
+            for v in range(2):
+                nc.tensor.matmul(
+                    out=pooled[:],
+                    lhsT=pool_and_repeat[:].rearrange("k c n -> k (c n)"),
+                    rhs=by_v[:, :, v],
+                    start=(v == 0),
+                    stop=(v == 1),
                 )
-                pooled = psum_out.tile([P, BANK], F32, tag="out_bank")
-                for v in range(2):
-                    nc.tensor.matmul(
-                        out=pooled[:],
-                        lhsT=pool_and_repeat[:].rearrange("k c n -> k (c n)"),
-                        rhs=by_v[:, :, v],
-                        start=(v == 0),
-                        stop=(v == 1),
-                    )
-                shortcut = work.tile([P, BANK], F32, tag="shortcut", bufs=4)
-                nc.scalar.activation(
-                    out=shortcut[:], in_=pooled[:], func=IDENTITY, bias=bias2_col[:, m : m + 1]
-                )
-                tiles.append(shortcut)
-            return tiles
+            shortcut = work.tile([P, BANK], F32, tag="shortcut", bufs=4)
+            nc.scalar.activation(out=shortcut[:], in_=pooled[:], func=IDENTITY, bias=bias2_col[:, m : m + 1])
+            return shortcut
 
-        def second_layer(r, o2_grouped, shortcuts):
-            b, half = divmod(r, ROUNDS_PER_IMAGE)
-            o2_codes = work.tile([P, HIDDEN_PASSES, ROUND], U32, align_bytes=64)
-            o2_scales = work.tile([P, HIDDEN_PASSES, ROUND], U8, align_bytes=64)
-            for g in range(HIDDEN_PASSES):
-                nc.vector.quantize_mx(
-                    out=o2_codes[:, g, :].bitcast(FP8X4),
-                    scales=o2_scales[:, g, :],
-                    in_=o2_grouped[g][:].rearrange("q n t -> q (n t)"),
-                )
-            sums = []
+        def quantise_o2(o2_grouped_half):
+            codes = work.tile([P, ROUND], U32, tag="o2_codes", bufs=4, align_bytes=64)
+            scales = work.tile([P, ROUND], U8, tag="o2_scales", bufs=4, align_bytes=64)
+            nc.vector.quantize_mx(
+                out=codes[:].bitcast(FP8X4),
+                scales=scales[:],
+                in_=o2_grouped_half[:].rearrange("q n t -> q (n t)"),
+            )
+            return codes, scales
+
+        def second_layer_pass(g, codes, scales, sums):
             for m in range(OUT_TILES):
-                o3 = psum_out.tile([P, BANK], F32, tag="out_bank")
-                sums.append(o3)
-            for g in range(HIDDEN_PASSES):
-                for m in range(OUT_TILES):
-                    nc.tensor.matmul_mx(
-                        out=sums[m][:],
-                        lhsT=w2_codes[:, g, m * P : (m + 1) * P].bitcast(FP8X4),
-                        lhsT_scale=w2_scales[:, g, m * P : (m + 1) * P],
-                        rhs=o2_codes[:, g, :].bitcast(FP8X4),
-                        rhs_scale=o2_scales[:, g, :],
-                        start=(g == 0),
-                        stop=(g == HIDDEN_PASSES - 1),
-                    )
-            for m in range(OUT_TILES):
-                result = work.tile([P, BANK], F32, tag="result", bufs=4)
-                nc.vector.tensor_tensor(out=result[:], in0=sums[m][:], in1=shortcuts[m][:], op=ADD)
-                nc.sync.dma_start(
-                    out=out[b, m * P : (m + 1) * P].rearrange("o i j -> o (i j)")[
-                        :, half * ROUND : (half + 1) * ROUND
-                    ],
-                    in_=result[:],
+                nc.tensor.matmul_mx(
+                    out=sums[m][:],
+                    lhsT=w2_codes[:, g, m * P : (m + 1) * P].bitcast(FP8X4),
+                    lhsT_scale=w2_scales[:, g, m * P : (m + 1) * P],
+                    rhs=codes[:].bitcast(FP8X4),
+                    rhs_scale=scales[:],
+                    start=(g == 0),
+                    stop=(g == HIDDEN_PASSES - 1),
                 )
 
-        o2_grouped = {}
-        shortcuts = {}
+        def finish(r, m, o3, shortcut):
+            b, half = divmod(r, ROUNDS_PER_IMAGE)
+            result = work.tile([P, BANK], F32, tag="result", bufs=4)
+            nc.vector.tensor_tensor(out=result[:], in0=o3[:], in1=shortcut[:], op=ADD)
+            nc.sync.dma_start(
+                out=out[b, m * P : (m + 1) * P].rearrange("o i j -> o (i j)")[
+                    :, half * ROUND : (half + 1) * ROUND
+                ],
+                in_=result[:],
+            )
+
+        patches = {}
         halves = {}
-        quantise_patches(0)
-        for tile_index in range(TOKEN_TILES + 2):
-            r, k = divmod(tile_index, TILES_PER_ROUND)
-            if tile_index < TOKEN_TILES:
-                halves[tile_index] = first_layer(tile_index)
-                if k == 1 and r + 1 < ROUNDS:
-                    quantise_patches(r + 1)
-            if 1 <= tile_index <= TOKEN_TILES:
-                before = tile_index - 1
+        o2_grouped = {}
+        o2_quantised = {}
+        shortcuts = {}
+        sums = {}
+
+        patches[0] = regroup_patches(0)
+        quantise_patches(0, patches[0])
+        spread_bias1()
+        for tile_index in range(1, REGROUP_AHEAD):
+            patches[tile_index] = regroup_patches(tile_index)
+        for tile_index in range(1, QUANTISE_AHEAD):
+            quantise_patches(tile_index, patches[tile_index])
+
+        for slot in range(SLOTS):
+            due = part_due(slot, RESIDUAL_LAG)
+            if due is not None:
+                shortcuts[due] = residual(due[0], due[1])
+            due = part_due(slot, SECOND_LAYER_LAG)
+            if due is not None:
+                r, g = due
+                if g == 0:
+                    sums[r] = [
+                        psum.tile([P, BANK], F32, name="o3_%d" % m, tag="o3", bufs=2) for m in range(OUT_TILES)
+                    ]
+                second_layer_pass(g, o2_quantised[due][0], o2_quantised[due][1], sums[r])
+
+            if slot < TOKEN_TILES:
+                halves[slot] = first_layer(slot)
+            if slot + QUANTISE_AHEAD < TOKEN_TILES:
+                quantise_patches(slot + QUANTISE_AHEAD, patches[slot + QUANTISE_AHEAD])
+
+            before = slot - ACTIVATE_LAG
+            if 0 <= before < TOKEN_TILES:
+                r = before // TILES_PER_ROUND
                 if before % TILES_PER_ROUND == 0:
-                    o2_grouped[before // TILES_PER_ROUND] = [
+                    o2_grouped[r] = [
                         work.tile([P, ROUND, PACK], BF16, name="o2_grouped_%d" % g, align_bytes=64)
                         for g in range(HIDDEN_PASSES)
                     ]
-                activate(before, halves[before], o2_grouped[before // TILES_PER_ROUND])
-                if before % TILES_PER_ROUND == TILES_PER_ROUND - 2:
-                    shortcuts[before // TILES_PER_ROUND] = residual(before // TILES_PER_ROUND)
-            if tile_index >= 2 and (tile_index - 2) % TILES_PER_ROUND == TILES_PER_ROUND - 1:
-                done = (tile_index - 2) // TILES_PER_ROUND
-                second_layer(done, o2_grouped[done], shortcuts[done])
+                activate(before, halves[before], o2_grouped[r])
+            if slot + REGROUP_AHEAD < TOKEN_TILES:
+                patches[slot + REGROUP_AHEAD] = regroup_patches(slot + REGROUP_AHEAD)
+
+            due = part_due(slot, QUANTISE_O2_LAG)
+            if due is not None:
+                o2_quantised[due] = quantise_o2(o2_grouped[due[0]][due[1]])
+            due = part_due(slot, FINISH_LAG)
+            if due is not None:
+                r, m = due
+                finish(r, m, sums[r][m], shortcuts[due])

@@ -25,11 +25,13 @@ TOKENS_PER_IMAGE = TOKENS // BATCH
 
 TOKEN_TILES = TOKENS // P
 TILES_PER_IMAGE = TOKEN_TILES // BATCH
+TILES_PER_LOAD = 2
 PATCH_ROWS = P // (WIDTH // 2)
 ROUND = BANK
 ROUNDS = TOKENS // ROUND
 ROUNDS_PER_IMAGE = ROUNDS // BATCH
 TILES_PER_ROUND = ROUND // P
+ROUND_PATCH_ROWS = ROUND // (WIDTH // 2)
 HIDDEN_PASSES = HIDDEN // K_PASS
 OUT_TILES = OUT_CHANNELS // P
 
@@ -38,17 +40,18 @@ FLOPS = 2 * TOKENS * (CHANNELS * PACK) * HIDDEN + 2 * TOKENS * HIDDEN * OUT_CHAN
 REGROUP_AHEAD = 3
 QUANTISE_AHEAD = 2
 ACTIVATE_LAG = 1
-RESIDUAL_LAG = 4
-QUANTISE_O2_LAG = 5
-SECOND_LAYER_LAG = 6
-FINISH_LAG = 7
-SLOTS = TILES_PER_ROUND * (ROUNDS - 1) + FINISH_LAG + 2
+POOL_SLOTS = (4, 6)
+QUANTISE_O2_SLOTS = (5, 6)
+SECOND_LAYER_SLOTS = (7, 9)
+FINISH_SLOTS = (8, 11)
+SLOTS = TILES_PER_ROUND * (ROUNDS - 1) + FINISH_SLOTS[1] + 1
 
 
-def part_due(slot, lag):
-    r, part = divmod(slot - lag, TILES_PER_ROUND)
-    if 0 <= r < ROUNDS and part < 2:
-        return r, part
+def part_due(slot, part_slots):
+    for part, lag in enumerate(part_slots):
+        r, rest = divmod(slot - lag, TILES_PER_ROUND)
+        if rest == 0 and 0 <= r < ROUNDS:
+            return r, part
     return None
 
 
@@ -62,44 +65,43 @@ def tile_memoryefficientpatchdownscale_kernel(
         psum = ctx.enter_context(tc.psum_pool(name="psum", bufs=2))
         ctx.enter_context(tc.manual_schedule())
 
-        w1_scales = keep.tile([P, HIDDEN], U8, align_bytes=64)
-        w2_scales = keep.tile([P, HIDDEN_PASSES, OUT_CHANNELS], U8, align_bytes=64)
-        nc.vector.memset(w1_scales[:].bitcast(I32), 0)
-        nc.vector.memset(w2_scales[:].rearrange("q g n -> q (g n)").bitcast(I32), 0)
-
-        bias1_row = keep.tile([P, HIDDEN], BF16)
-        ones = keep.tile([P, P], BF16)
-        nc.vector.memset(bias1_row[:], 0.0)
-        nc.vector.memset(ones[:], 1.0)
-        nc.scalar.dma_start(out=bias1_row[0:1, :], in_=bias1.unsqueeze(0))
-        bias2_col = keep.tile([P, OUT_TILES], BF16)
-        with nc.allow_non_contiguous_dma(reason="256 bias values, one to a partition"):
-            nc.scalar.dma_start(out=bias2_col[:], in_=bias2.rearrange("(m r) -> r m", r=P))
-
         table_in = keep.tile([P, 1], F32)
         table_out = keep.tile([P, 1], F32)
         nc.vector.memset(table_in[:], 0.0)
         nc.scalar.activation(out=table_out[:], in_=table_in[:], func=SILU)
 
+        w1_scales = keep.tile([P, HIDDEN], U8, align_bytes=64)
+        w2_scales = keep.tile([P, HIDDEN_PASSES, OUT_CHANNELS], U8, align_bytes=64)
+        bias1_row = keep.tile([P, HIDDEN], BF16)
+        ones = keep.tile([P, P], BF16)
+        nc.vector.memset(bias1_row[:], 0.0)
+        nc.vector.memset(w1_scales[:].bitcast(I32), 0)
+        nc.vector.memset(w2_scales[:].rearrange("q g n -> q (g n)").bitcast(I32), 0)
+        nc.vector.memset(ones[:], 1.0)
+        bias2_col = keep.tile([P, OUT_TILES], BF16)
+
         x_rows = keep.tile([P, TOKEN_TILES, PACK * P], BF16)
-        x_pairs = keep.tile([P, OUT_TILES, BATCH, TOKENS_PER_IMAGE * 2], BF16)
+        x_twice = {}
         w1_codes = keep.tile([P, HIDDEN], U32, align_bytes=64)
         w2_codes = keep.tile([P, HIDDEN_PASSES, OUT_CHANNELS], U32, align_bytes=64)
 
-        def load_x_rows(tile_index):
-            b, k = divmod(tile_index, TILES_PER_IMAGE)
+        def load_x_rows(first_tile):
+            b, k = divmod(first_tile, TILES_PER_IMAGE)
             image = x[b].rearrange("c h w -> c (h w)")
             nc.sync.dma_start(
-                out=x_rows[:, tile_index, :], in_=image[:, k * PACK * P : (k + 1) * PACK * P]
+                out=x_rows[:, first_tile : first_tile + TILES_PER_LOAD, :].rearrange("c k e -> c (k e)"),
+                in_=image[:, k * PACK * P : (k + TILES_PER_LOAD) * PACK * P],
             )
 
-        def load_x_pairs(b):
+        def load_x_twice(b):
             for m in range(OUT_TILES):
-                channels = x[b, m * (P // 2) : (m + 1) * (P // 2)].rearrange("c (i u) w -> u c i w", u=2)
+                x_twice[(b, m)] = keep.tile([P, HEIGHT * WIDTH], BF16, name="x_twice_%d_%d" % (b, m))
                 for u in range(2):
                     nc.sync.dma_start(
-                        out=x_pairs[u:P:2, m, b, :].rearrange("k (i w) -> k i w", w=WIDTH),
-                        in_=channels[u],
+                        out=x_twice[(b, m)][u:P:2, 0 : (HEIGHT - 1) * WIDTH],
+                        in_=x[b, m * (P // 2) : (m + 1) * (P // 2), u : u + HEIGHT - 1, :].rearrange(
+                            "c h w -> c (h w)"
+                        ),
                     )
 
         def load_weight1():
@@ -130,14 +132,17 @@ def tile_memoryefficientpatchdownscale_kernel(
                 )
 
         load_x_rows(0)
+        nc.sync.dma_start(out=bias1_row[0:1, :], in_=bias1.unsqueeze(0))
         load_weight1()
-        for tile_index in range(1, TILES_PER_IMAGE):
-            load_x_rows(tile_index)
-        load_x_pairs(0)
+        for first_tile in range(TILES_PER_LOAD, TILES_PER_IMAGE, TILES_PER_LOAD):
+            load_x_rows(first_tile)
+        load_x_twice(0)
         load_weight2()
-        for tile_index in range(TILES_PER_IMAGE, TOKEN_TILES):
-            load_x_rows(tile_index)
-        load_x_pairs(1)
+        with nc.allow_non_contiguous_dma(reason="256 bias values, one to a partition"):
+            nc.sync.dma_start(out=bias2_col[:], in_=bias2.rearrange("(m r) -> r m", r=P))
+        for first_tile in range(TILES_PER_IMAGE, TOKEN_TILES, TILES_PER_LOAD):
+            load_x_rows(first_tile)
+        load_x_twice(1)
 
         identity = keep.tile([P, P], F32)
         make_identity(nc, identity[:])
@@ -222,20 +227,22 @@ def tile_memoryefficientpatchdownscale_kernel(
                     func=SILU,
                 )
 
-        def residual(r, m):
+        def pool(r, m):
             b, half = divmod(r, ROUNDS_PER_IMAGE)
-            by_v = x_pairs[:, m, b, half * 2 * ROUND : (half + 1) * 2 * ROUND].rearrange(
-                "k (n v) -> k n v", v=2
-            )
+            rows = slice(half * ROUND_PATCH_ROWS, (half + 1) * ROUND_PATCH_ROWS)
+            image = x_twice[(b, m)][:].rearrange("k (i u j v) -> k i u j v", u=2, j=WIDTH // 2, v=2)
             pooled = psum.tile([P, BANK], F32, tag="pooled", bufs=1)
             for v in range(2):
                 nc.tensor.matmul(
-                    out=pooled[:],
+                    out=pooled[:].rearrange("o (i j) -> o i j", j=WIDTH // 2),
                     lhsT=pool_and_repeat[:].rearrange("k c n -> k (c n)"),
-                    rhs=by_v[:, :, v],
+                    rhs=image[:, rows, 0, :, v],
                     start=(v == 0),
                     stop=(v == 1),
                 )
+            return pooled
+
+        def add_bias2(m, pooled):
             shortcut = work.tile([P, BANK], F32, tag="shortcut", bufs=4)
             nc.scalar.activation(out=shortcut[:], in_=pooled[:], func=IDENTITY, bias=bias2_col[:, m : m + 1])
             return shortcut
@@ -250,10 +257,12 @@ def tile_memoryefficientpatchdownscale_kernel(
             )
             return codes, scales
 
-        def second_layer_pass(g, codes, scales, sums):
-            for m in range(OUT_TILES):
+        def second_layer(m, quantised_halves):
+            o3 = psum.tile([P, BANK], F32, tag="o3", bufs=2)
+            for g in range(HIDDEN_PASSES):
+                codes, scales = quantised_halves[g]
                 nc.tensor.matmul_mx(
-                    out=sums[m][:],
+                    out=o3[:],
                     lhsT=w2_codes[:, g, m * P : (m + 1) * P].bitcast(FP8X4),
                     lhsT_scale=w2_scales[:, g, m * P : (m + 1) * P],
                     rhs=codes[:].bitcast(FP8X4),
@@ -261,6 +270,7 @@ def tile_memoryefficientpatchdownscale_kernel(
                     start=(g == 0),
                     stop=(g == HIDDEN_PASSES - 1),
                 )
+            return o3
 
         def finish(r, m, o3, shortcut):
             b, half = divmod(r, ROUNDS_PER_IMAGE)
@@ -289,22 +299,24 @@ def tile_memoryefficientpatchdownscale_kernel(
             quantise_patches(tile_index, patches[tile_index])
 
         for slot in range(SLOTS):
-            due = part_due(slot, RESIDUAL_LAG)
+            due = part_due(slot, QUANTISE_O2_SLOTS)
             if due is not None:
-                shortcuts[due] = residual(due[0], due[1])
-            due = part_due(slot, SECOND_LAYER_LAG)
+                o2_quantised[due] = quantise_o2(o2_grouped[due[0]][due[1]])
+            due = part_due(slot, FINISH_SLOTS)
             if due is not None:
-                r, g = due
-                if g == 0:
-                    sums[r] = [
-                        psum.tile([P, BANK], F32, name="o3_%d" % m, tag="o3", bufs=2) for m in range(OUT_TILES)
-                    ]
-                second_layer_pass(g, o2_quantised[due][0], o2_quantised[due][1], sums[r])
+                finish(due[0], due[1], sums[due], shortcuts[due])
 
             if slot < TOKEN_TILES:
                 halves[slot] = first_layer(slot)
             if slot + QUANTISE_AHEAD < TOKEN_TILES:
                 quantise_patches(slot + QUANTISE_AHEAD, patches[slot + QUANTISE_AHEAD])
+
+            pool_due = part_due(slot, POOL_SLOTS)
+            if pool_due is not None:
+                pooled = pool(pool_due[0], pool_due[1])
+            due = part_due(slot, SECOND_LAYER_SLOTS)
+            if due is not None:
+                sums[due] = second_layer(due[1], [o2_quantised[(due[0], g)] for g in range(HIDDEN_PASSES)])
 
             before = slot - ACTIVATE_LAG
             if 0 <= before < TOKEN_TILES:
@@ -317,11 +329,5 @@ def tile_memoryefficientpatchdownscale_kernel(
                 activate(before, halves[before], o2_grouped[r])
             if slot + REGROUP_AHEAD < TOKEN_TILES:
                 patches[slot + REGROUP_AHEAD] = regroup_patches(slot + REGROUP_AHEAD)
-
-            due = part_due(slot, QUANTISE_O2_LAG)
-            if due is not None:
-                o2_quantised[due] = quantise_o2(o2_grouped[due[0]][due[1]])
-            due = part_due(slot, FINISH_LAG)
-            if due is not None:
-                r, m = due
-                finish(r, m, sums[r][m], shortcuts[due])
+            if pool_due is not None:
+                shortcuts[pool_due] = add_bias2(pool_due[1], pooled)

@@ -40,7 +40,8 @@ FLOPS = 2 * TOKENS * (CHANNELS * PACK) * HIDDEN + 2 * TOKENS * HIDDEN * OUT_CHAN
 REGROUP_AHEAD = 3
 QUANTISE_AHEAD = 2
 ACTIVATE_LAG = 1
-POOL_SLOTS = (4, 6)
+POOL_SLOTS = (2, 4)
+ADD_BIAS2_SLOTS = (3, 5)
 QUANTISE_O2_SLOTS = (5, 6)
 SECOND_LAYER_SLOTS = (7, 9)
 FINISH_SLOTS = (8, 11)
@@ -180,7 +181,7 @@ def tile_memoryefficientpatchdownscale_kernel(
 
         def spread_bias1():
             for g in range(HIDDEN_PASSES):
-                bias1_rep = psum.tile([P, BANK], F32, tag="pooled", bufs=1)
+                bias1_rep = psum.tile([P, BANK], F32, tag="means", bufs=1)
                 nc.tensor.matmul(
                     out=bias1_rep[:],
                     lhsT=ones[:],
@@ -231,20 +232,20 @@ def tile_memoryefficientpatchdownscale_kernel(
             b, half = divmod(r, ROUNDS_PER_IMAGE)
             rows = slice(half * ROUND_PATCH_ROWS, (half + 1) * ROUND_PATCH_ROWS)
             image = x_twice[(b, m)][:].rearrange("k (i u j v) -> k i u j v", u=2, j=WIDTH // 2, v=2)
-            pooled = psum.tile([P, BANK], F32, tag="pooled", bufs=1)
+            means = psum.tile([P, BANK], F32, tag="means", bufs=1)
             for v in range(2):
                 nc.tensor.matmul(
-                    out=pooled[:].rearrange("o (i j) -> o i j", j=WIDTH // 2),
+                    out=means[:].rearrange("o (i j) -> o i j", j=WIDTH // 2),
                     lhsT=pool_and_repeat[:].rearrange("k c n -> k (c n)"),
                     rhs=image[:, rows, 0, :, v],
                     start=(v == 0),
                     stop=(v == 1),
                 )
-            return pooled
+            return means
 
-        def add_bias2(m, pooled):
+        def add_bias2(m, means):
             shortcut = work.tile([P, BANK], F32, tag="shortcut", bufs=4)
-            nc.scalar.activation(out=shortcut[:], in_=pooled[:], func=IDENTITY, bias=bias2_col[:, m : m + 1])
+            nc.scalar.activation(out=shortcut[:], in_=means[:], func=IDENTITY, bias=bias2_col[:, m : m + 1])
             return shortcut
 
         def quantise_o2(o2_grouped_half):
@@ -287,6 +288,7 @@ def tile_memoryefficientpatchdownscale_kernel(
         halves = {}
         o2_grouped = {}
         o2_quantised = {}
+        pooled = {}
         shortcuts = {}
         sums = {}
 
@@ -299,6 +301,10 @@ def tile_memoryefficientpatchdownscale_kernel(
             quantise_patches(tile_index, patches[tile_index])
 
         for slot in range(SLOTS):
+            if slot < TOKEN_TILES:
+                halves[slot] = first_layer(slot)
+            if slot + QUANTISE_AHEAD < TOKEN_TILES:
+                quantise_patches(slot + QUANTISE_AHEAD, patches[slot + QUANTISE_AHEAD])
             due = part_due(slot, QUANTISE_O2_SLOTS)
             if due is not None:
                 o2_quantised[due] = quantise_o2(o2_grouped[due[0]][due[1]])
@@ -306,18 +312,9 @@ def tile_memoryefficientpatchdownscale_kernel(
             if due is not None:
                 finish(due[0], due[1], sums[due], shortcuts[due])
 
-            if slot < TOKEN_TILES:
-                halves[slot] = first_layer(slot)
-            if slot + QUANTISE_AHEAD < TOKEN_TILES:
-                quantise_patches(slot + QUANTISE_AHEAD, patches[slot + QUANTISE_AHEAD])
-
-            pool_due = part_due(slot, POOL_SLOTS)
-            if pool_due is not None:
-                pooled = pool(pool_due[0], pool_due[1])
-            due = part_due(slot, SECOND_LAYER_SLOTS)
+            due = part_due(slot, ADD_BIAS2_SLOTS)
             if due is not None:
-                sums[due] = second_layer(due[1], [o2_quantised[(due[0], g)] for g in range(HIDDEN_PASSES)])
-
+                shortcuts[due] = add_bias2(due[1], pooled[due])
             before = slot - ACTIVATE_LAG
             if 0 <= before < TOKEN_TILES:
                 r = before // TILES_PER_ROUND
@@ -329,5 +326,10 @@ def tile_memoryefficientpatchdownscale_kernel(
                 activate(before, halves[before], o2_grouped[r])
             if slot + REGROUP_AHEAD < TOKEN_TILES:
                 patches[slot + REGROUP_AHEAD] = regroup_patches(slot + REGROUP_AHEAD)
-            if pool_due is not None:
-                shortcuts[pool_due] = add_bias2(pool_due[1], pooled)
+
+            due = part_due(slot, POOL_SLOTS)
+            if due is not None:
+                pooled[due] = pool(due[0], due[1])
+            due = part_due(slot, SECOND_LAYER_SLOTS)
+            if due is not None:
+                sums[due] = second_layer(due[1], [o2_quantised[(due[0], g)] for g in range(HIDDEN_PASSES)])

@@ -15,51 +15,41 @@ IDENTITY = mybir.ActivationFunctionType.Identity
 
 P = 128
 PACK = 4
-K_PASS = P * PACK
 BANK = 512
 
 BATCH, CHANNELS, HEIGHT, WIDTH = 2, 128, 64, 64
 HIDDEN, OUT_CHANNELS = 1024, 256
-TOKENS = BATCH * (HEIGHT // 2) * (WIDTH // 2)
-TOKENS_PER_IMAGE = TOKENS // BATCH
-
-TOKEN_TILES = TOKENS // P
-TILES_PER_IMAGE = TOKEN_TILES // BATCH
-TILES_PER_LOAD = 2
-PATCH_ROWS = P // (WIDTH // 2)
-ROUND = BANK
-ROUNDS = TOKENS // ROUND
-ROUNDS_PER_IMAGE = ROUNDS // BATCH
-TILES_PER_ROUND = ROUND // P
-ROUND_PATCH_ROWS = ROUND // (WIDTH // 2)
-HIDDEN_PASSES = HIDDEN // K_PASS
-OUT_TILES = OUT_CHANNELS // P
+PATCH_COLS = WIDTH // 2
+TOKENS_PER_IMAGE = (HEIGHT // 2) * PATCH_COLS
+TOKENS = BATCH * TOKENS_PER_IMAGE
+HALVES = HIDDEN // (P * PACK)
+REPEAT = OUT_CHANNELS // CHANNELS
 
 FLOPS = 2 * TOKENS * (CHANNELS * PACK) * HIDDEN + 2 * TOKENS * HIDDEN * OUT_CHANNELS
 
-REGROUP_AHEAD = 3
-QUANTISE_AHEAD = 2
-ACTIVATE_LAG = 1
-POOL_SLOTS = (2, 4)
-ADD_BIAS2_SLOTS = (3, 5)
-QUANTISE_O2_SLOTS = (5, 6)
-SECOND_LAYER_SLOTS = (7, 9)
-FINISH_SLOTS = (8, 11)
-SLOTS = TILES_PER_ROUND * (ROUNDS - 1) + FINISH_SLOTS[1] + 1
-
-
-def part_due(slot, part_slots):
-    for part, lag in enumerate(part_slots):
-        r, rest = divmod(slot - lag, TILES_PER_ROUND)
-        if rest == 0 and 0 <= r < ROUNDS:
-            return r, part
-    return None
+CHUNKS = (256, 512, 512, 512, 256)
+LEAD = 5
+REGROUP_ON_SCALAR = (0,)
 
 
 def tile_memoryefficientpatchdownscale_kernel(
     tc, x, weight1_words, weight1_scales, bias1, weight2_words, weight2_scales, bias2, out
 ):
     nc = tc.nc
+    starts = [sum(CHUNKS[:c]) for c in range(len(CHUNKS))]
+    n_chunks = len(CHUNKS)
+
+    def image_parts(c):
+        parts = []
+        first, count = starts[c], CHUNKS[c]
+        while count > 0:
+            b, s = divmod(first, TOKENS_PER_IMAGE)
+            take = min(count, TOKENS_PER_IMAGE - s)
+            parts.append((b, s, first - starts[c], take))
+            first += take
+            count -= take
+        return parts
+
     with ExitStack() as ctx:
         keep = ctx.enter_context(tc.tile_pool(name="keep", bufs=1))
         work = ctx.enter_context(tc.tile_pool(name="work", bufs=2))
@@ -71,265 +61,273 @@ def tile_memoryefficientpatchdownscale_kernel(
         nc.vector.memset(table_in[:], 0.0)
         nc.scalar.activation(out=table_out[:], in_=table_in[:], func=SILU)
 
-        w1_scales = keep.tile([P, HIDDEN], U8, align_bytes=64)
-        w2_scales = keep.tile([P, HIDDEN_PASSES, OUT_CHANNELS], U8, align_bytes=64)
-        bias1_row = keep.tile([P, HIDDEN], BF16)
-        ones = keep.tile([P, P], BF16)
-        nc.vector.memset(bias1_row[:], 0.0)
-        nc.vector.memset(w1_scales[:].bitcast(I32), 0)
-        nc.vector.memset(w2_scales[:].rearrange("q g n -> q (g n)").bitcast(I32), 0)
-        nc.vector.memset(ones[:], 1.0)
-        bias2_col = keep.tile([P, OUT_TILES], BF16)
+        w1_scales_raw = keep.tile([P, HIDDEN], U8, align_bytes=64)
+        w2_scales_raw = keep.tile([P, HALVES, OUT_CHANNELS], U8, align_bytes=64)
+        nc.vector.memset(w1_scales_raw[:].bitcast(I32), 0)
+        nc.vector.memset(w2_scales_raw[:].rearrange("q g n -> q (g n)").bitcast(I32), 0)
+        w1_codes_raw = keep.tile([P, HIDDEN], I32, align_bytes=64)
+        w2_codes_raw = keep.tile([P, HALVES, OUT_CHANNELS], I32, align_bytes=64)
+        w1_codes = keep.tile([P, HALVES, PACK, P], I32, align_bytes=64)
+        w1_scales = keep.tile([P, HALVES, PACK, P], U8, align_bytes=64)
+        w2_codes = keep.tile([P, HALVES, REPEAT, P], I32, align_bytes=64)
+        w2_scales = keep.tile([P, HALVES, REPEAT, P], U8, align_bytes=64)
+        bias1_col = keep.tile([P, HALVES, PACK], BF16)
+        bias2_col = keep.tile([P, REPEAT], BF16)
+        x_rows = keep.tile([P, BATCH * HEIGHT * WIDTH], BF16)
+        p_codes = keep.tile([P, TOKENS], U32, align_bytes=64)
+        p_scales = keep.tile([P, TOKENS], U8, align_bytes=64)
 
-        x_rows = keep.tile([P, TOKEN_TILES, PACK * P], BF16)
-        x_twice = {}
-        w1_codes = keep.tile([P, HIDDEN], U32, align_bytes=64)
-        w2_codes = keep.tile([P, HIDDEN_PASSES, OUT_CHANNELS], U32, align_bytes=64)
+        def load_x(c):
+            for b, s, offset, count in image_parts(c):
+                first = starts[c] + offset
+                nc.sync.dma_start(
+                    out=x_rows[:, PACK * first : PACK * (first + count)],
+                    in_=x[b].rearrange("c h w -> c (h w)")[:, PACK * s : PACK * (s + count)],
+                )
 
-        def load_x_rows(first_tile):
-            b, k = divmod(first_tile, TILES_PER_IMAGE)
-            image = x[b].rearrange("c h w -> c (h w)")
+        load_x(0)
+        with nc.allow_non_contiguous_dma(reason="bias values, four or two to a partition"):
+            nc.sync.dma_start(out=bias1_col[:], in_=bias1.rearrange("(g q t) -> q g t", g=HALVES, t=PACK))
+        for quadrant in range(4):
             nc.sync.dma_start(
-                out=x_rows[:, first_tile : first_tile + TILES_PER_LOAD, :].rearrange("c k e -> c (k e)"),
-                in_=image[:, k * PACK * P : (k + TILES_PER_LOAD) * PACK * P],
+                out=w1_scales_raw[32 * quadrant : 32 * quadrant + 4, :].bitcast(I32),
+                in_=weight1_scales[0, 4 * quadrant : 4 * quadrant + 4, :].bitcast(I32),
             )
+        w1_bytes = weight1_words[0].rearrange("p n t -> p (n t)").bitcast(I32)
+        for g in range(HALVES):
+            nc.sync.dma_start(
+                out=w1_codes_raw[:, g * BANK : (g + 1) * BANK], in_=w1_bytes[:, g * BANK : (g + 1) * BANK]
+            )
+        load_x(1)
+        load_x(2)
+        for quadrant in range(4):
+            nc.sync.dma_start(
+                out=w2_scales_raw[32 * quadrant : 32 * quadrant + 4, :, :].bitcast(I32),
+                in_=weight2_scales[:, 4 * quadrant : 4 * quadrant + 4, :].rearrange("g r n -> r g n").bitcast(I32),
+            )
+        for g in range(HALVES):
+            nc.sync.dma_start(
+                out=w2_codes_raw[:, g, :], in_=weight2_words[g].rearrange("p n t -> p (n t)").bitcast(I32)
+            )
+        with nc.allow_non_contiguous_dma(reason="bias values, four or two to a partition"):
+            nc.sync.dma_start(out=bias2_col[:], in_=bias2.rearrange("(c e) -> c e", e=REPEAT))
+        for c in range(3, n_chunks):
+            load_x(c)
 
-        def load_x_twice(b):
-            for m in range(OUT_TILES):
-                x_twice[(b, m)] = keep.tile([P, HEIGHT * WIDTH], BF16, name="x_twice_%d_%d" % (b, m))
-                for u in range(2):
-                    nc.sync.dma_start(
-                        out=x_twice[(b, m)][u:P:2, 0 : (HEIGHT - 1) * WIDTH],
-                        in_=x[b, m * (P // 2) : (m + 1) * (P // 2), u : u + HEIGHT - 1, :].rearrange(
-                            "c h w -> c (h w)"
-                        ),
-                    )
-
-        def load_weight1():
-            for quadrant in range(4):
-                nc.sync.dma_start(
-                    out=w1_scales[32 * quadrant : 32 * quadrant + 4, :].bitcast(I32),
-                    in_=weight1_scales[0, 4 * quadrant : 4 * quadrant + 4, :].bitcast(I32),
-                )
-            w1_bytes = weight1_words[0].rearrange("p n t -> p (n t)").bitcast(I32)
-            for g in range(HIDDEN_PASSES):
-                nc.sync.dma_start(
-                    out=w1_codes[:, g * BANK : (g + 1) * BANK].bitcast(I32),
-                    in_=w1_bytes[:, g * BANK : (g + 1) * BANK],
-                )
-
-        def load_weight2():
-            for quadrant in range(4):
-                nc.sync.dma_start(
-                    out=w2_scales[32 * quadrant : 32 * quadrant + 4, :, :].bitcast(I32),
-                    in_=weight2_scales[:, 4 * quadrant : 4 * quadrant + 4, :]
-                    .rearrange("g r n -> r g n")
-                    .bitcast(I32),
-                )
-            for g in range(HIDDEN_PASSES):
-                nc.sync.dma_start(
-                    out=w2_codes[:, g, :].bitcast(I32),
-                    in_=weight2_words[g].rearrange("p n t -> p (n t)").bitcast(I32),
-                )
-
-        load_x_rows(0)
-        nc.sync.dma_start(out=bias1_row[0:1, :], in_=bias1.unsqueeze(0))
-        load_weight1()
-        for first_tile in range(TILES_PER_LOAD, TILES_PER_IMAGE, TILES_PER_LOAD):
-            load_x_rows(first_tile)
-        load_x_twice(0)
-        load_weight2()
-        with nc.allow_non_contiguous_dma(reason="256 bias values, one to a partition"):
-            nc.sync.dma_start(out=bias2_col[:], in_=bias2.rearrange("(m r) -> r m", r=P))
-        for first_tile in range(TILES_PER_IMAGE, TOKEN_TILES, TILES_PER_LOAD):
-            load_x_rows(first_tile)
-        load_x_twice(1)
-
-        identity = keep.tile([P, P], F32)
+        identity = keep.tile([P, P], BF16)
         make_identity(nc, identity[:])
 
-        identity_pairs = identity[:].rearrange("k (c n) -> k c n", n=2)
-        same_channel = keep.tile([P, P // 2], F32)
-        pool_and_repeat = keep.tile([P, P // 2, 2], BF16)
-        nc.vector.tensor_tensor(
-            out=same_channel[:], in0=identity_pairs[:, :, 0], in1=identity_pairs[:, :, 1], op=ADD
-        )
-        nc.vector.tensor_scalar_mul(
-            out=pool_and_repeat[:],
-            in0=same_channel[:].unsqueeze(2).to_broadcast([P, P // 2, 2]),
-            scalar1=0.25,
-        )
-
-        p_codes = keep.tile([P, TOKEN_TILES, P], U32, align_bytes=64)
-        p_scales = keep.tile([P, TOKEN_TILES, P], U8, align_bytes=64)
-        bias1_sorted = keep.tile([P, HIDDEN_PASSES, PACK, P], F32)
-
-        def regroup_patches(tile_index):
-            patches = work.tile([P, PACK * P], BF16, tag="patches", bufs=4, align_bytes=64)
-            nc.scalar.copy(
-                out=patches[:].bitcast(F32).rearrange("c (i j u) -> c i j u", i=PATCH_ROWS, u=2),
-                in_=x_rows[:, tile_index, :].bitcast(F32).rearrange("c (i u j) -> c i j u", i=PATCH_ROWS, u=2),
-            )
-            return patches
-
-        def quantise_patches(tile_index, patches):
-            nc.vector.quantize_mx(
-                out=p_codes[:, tile_index, :].bitcast(FP8X4),
-                scales=p_scales[:, tile_index, :],
-                in_=patches[:],
+        def sort_w1_scales(g):
+            nc.vector.tensor_copy(
+                out=w1_scales[:, g].rearrange("q t m -> q m t"),
+                in_=w1_scales_raw[:, g * BANK : (g + 1) * BANK].rearrange("q (m t) -> q m t", t=PACK),
             )
 
-        def spread_bias1():
-            for g in range(HIDDEN_PASSES):
-                bias1_rep = psum.tile([P, BANK], F32, tag="means", bufs=1)
-                nc.tensor.matmul(
-                    out=bias1_rep[:],
-                    lhsT=ones[:],
-                    rhs=bias1_row[:, g * BANK : (g + 1) * BANK],
-                    start=True,
-                    stop=True,
-                )
-                nc.scalar.copy(
-                    out=bias1_sorted[:, g], in_=bias1_rep[:].rearrange("n (q t) -> n t q", t=PACK)
-                )
-
-        def first_layer(tile_index):
-            halves = []
-            for g in range(HIDDEN_PASSES):
-                o1 = psum.tile([P, BANK], F32, tag="o1", bufs=2)
-                nc.tensor.matmul_mx(
-                    out=o1[:],
-                    lhsT=p_codes[:, tile_index, :].bitcast(FP8X4),
-                    lhsT_scale=p_scales[:, tile_index, :],
-                    rhs=w1_codes[:, g * BANK : (g + 1) * BANK].bitcast(FP8X4),
-                    rhs_scale=w1_scales[:, g * BANK : (g + 1) * BANK],
-                    start=True,
-                    stop=True,
-                )
-                o1_sorted = work.tile([P, PACK, P], F32, tag="o1_sorted", bufs=6)
-                nc.vector.tensor_tensor(
-                    out=o1_sorted[:],
-                    in0=o1[:].rearrange("n (q t) -> n t q", t=PACK),
-                    in1=bias1_sorted[:, g],
-                    op=ADD,
-                )
-                halves.append(o1_sorted)
-            return halves
-
-        def activate(tile_index, halves, o2_grouped):
-            k = tile_index % TILES_PER_ROUND
-            for g in range(HIDDEN_PASSES):
-                o1_t = psum.tile([P, PACK, P], F32, tag="o1_t", bufs=3)
-                for t in range(PACK):
-                    nc.tensor.transpose(o1_t[:, t, :], halves[g][:, t, :], identity[:])
-                nc.scalar.activation(
-                    out=o2_grouped[g][:, k * P : (k + 1) * P, :],
-                    in_=o1_t[:].rearrange("q t n -> q n t"),
-                    func=SILU,
-                )
-
-        def pool(r, m):
-            b, half = divmod(r, ROUNDS_PER_IMAGE)
-            rows = slice(half * ROUND_PATCH_ROWS, (half + 1) * ROUND_PATCH_ROWS)
-            image = x_twice[(b, m)][:].rearrange("k (i u j v) -> k i u j v", u=2, j=WIDTH // 2, v=2)
-            means = psum.tile([P, BANK], F32, tag="means", bufs=1)
-            for v in range(2):
-                nc.tensor.matmul(
-                    out=means[:].rearrange("o (i j) -> o i j", j=WIDTH // 2),
-                    lhsT=pool_and_repeat[:].rearrange("k c n -> k (c n)"),
-                    rhs=image[:, rows, 0, :, v],
-                    start=(v == 0),
-                    stop=(v == 1),
-                )
-            return means
-
-        def add_bias2(m, means):
-            shortcut = work.tile([P, BANK], F32, tag="shortcut", bufs=4)
-            nc.scalar.activation(out=shortcut[:], in_=means[:], func=IDENTITY, bias=bias2_col[:, m : m + 1])
-            return shortcut
-
-        def quantise_o2(o2_grouped_half):
-            codes = work.tile([P, ROUND], U32, tag="o2_codes", bufs=4, align_bytes=64)
-            scales = work.tile([P, ROUND], U8, tag="o2_scales", bufs=4, align_bytes=64)
-            nc.vector.quantize_mx(
-                out=codes[:].bitcast(FP8X4),
-                scales=scales[:],
-                in_=o2_grouped_half[:].rearrange("q n t -> q (n t)"),
+        def sort_w1_codes(g):
+            nc.vector.tensor_copy(
+                out=w1_codes[:, g],
+                in_=w1_codes_raw[:, g * BANK : (g + 1) * BANK].rearrange("p (m t) -> p t m", t=PACK),
             )
-            return codes, scales
 
-        def second_layer(m, quantised_halves):
-            o3 = psum.tile([P, BANK], F32, tag="o3", bufs=2)
-            for g in range(HIDDEN_PASSES):
-                codes, scales = quantised_halves[g]
-                nc.tensor.matmul_mx(
-                    out=o3[:],
-                    lhsT=w2_codes[:, g, m * P : (m + 1) * P].bitcast(FP8X4),
-                    lhsT_scale=w2_scales[:, g, m * P : (m + 1) * P],
-                    rhs=codes[:].bitcast(FP8X4),
-                    rhs_scale=scales[:],
-                    start=(g == 0),
-                    stop=(g == HIDDEN_PASSES - 1),
-                )
-            return o3
+        def sort_w2_codes():
+            nc.vector.tensor_copy(
+                out=w2_codes[:], in_=w2_codes_raw[:].rearrange("p g (c e) -> p g e c", e=REPEAT)
+            )
 
-        def finish(r, m, o3, shortcut):
-            b, half = divmod(r, ROUNDS_PER_IMAGE)
-            result = work.tile([P, BANK], F32, tag="result", bufs=4)
-            nc.vector.tensor_tensor(out=result[:], in0=o3[:], in1=shortcut[:], op=ADD)
-            nc.sync.dma_start(
-                out=out[b, m * P : (m + 1) * P].rearrange("o i j -> o (i j)")[
-                    :, half * ROUND : (half + 1) * ROUND
-                ],
-                in_=result[:],
+        def sort_w2_scales():
+            nc.vector.tensor_copy(
+                out=w2_scales[:].rearrange("q g e c -> q g c e"),
+                in_=w2_scales_raw[:].rearrange("q g (c e) -> q g c e", e=REPEAT),
             )
 
         patches = {}
-        halves = {}
+
+        def regroup(c):
+            first, count = starts[c], CHUNKS[c]
+            grouped = work.tile([P, PACK * count], BF16, tag="patches", bufs=2, align_bytes=64)
+            patches[c] = grouped
+            dst = grouped[:].bitcast(F32).rearrange("c (i j u) -> c i j u", j=PATCH_COLS, u=2)
+            src = (
+                x_rows[:, PACK * first : PACK * (first + count)]
+                .bitcast(F32)
+                .rearrange("c (i u j) -> c i j u", u=2, j=PATCH_COLS)
+            )
+            if c in REGROUP_ON_SCALAR:
+                nc.scalar.copy(out=dst, in_=src)
+            else:
+                nc.vector.tensor_copy(out=dst, in_=src)
+
+        def quantise_patches(c):
+            first, count = starts[c], CHUNKS[c]
+            nc.vector.quantize_mx(
+                out=p_codes[:, first : first + count].bitcast(FP8X4),
+                scales=p_scales[:, first : first + count],
+                in_=patches[c][:],
+            )
+
+        o1_banks = {}
+
+        def first_layer(c, g, t):
+            first, count = starts[c], CHUNKS[c]
+            o1 = psum.tile([P, BANK], F32, tag="o1", bufs=LEAD)
+            o1_banks[(c, g, t)] = o1
+            nc.tensor.matmul_mx(
+                out=o1[:, :count],
+                lhsT=w1_codes[:, g, t, :].bitcast(FP8X4),
+                lhsT_scale=w1_scales[:, g, t, :],
+                rhs=p_codes[:, first : first + count].bitcast(FP8X4),
+                rhs_scale=p_scales[:, first : first + count],
+                start=True,
+                stop=True,
+            )
+
+        o2_rows = {}
+
+        def silu(c, g, t):
+            count = CHUNKS[c]
+            if t == 0:
+                rows = work.tile([P, PACK, count], BF16, tag="o2_rows", bufs=3)
+                o2_rows[(c, g)] = rows
+            nc.scalar.activation(
+                out=o2_rows[(c, g)][:, t, :],
+                in_=o1_banks[(c, g, t)][:, :count],
+                func=SILU,
+                bias=bias1_col[:, g, t : t + 1],
+            )
+
         o2_grouped = {}
+
+        def interleave(c, g):
+            grouped = work.tile([P, CHUNKS[c], PACK], BF16, tag="o2_grouped", bufs=2, align_bytes=64)
+            o2_grouped[(c, g)] = grouped
+            nc.vector.tensor_copy(out=grouped[:], in_=o2_rows[(c, g)][:].rearrange("q t n -> q n t"))
+
         o2_quantised = {}
-        pooled = {}
-        shortcuts = {}
+
+        def quantise_o2(c, g):
+            codes = work.tile([P, CHUNKS[c]], U32, tag="o2_codes", bufs=4, align_bytes=64)
+            scales = work.tile([P, CHUNKS[c]], U8, tag="o2_scales", bufs=4, align_bytes=64)
+            o2_quantised[(c, g)] = (codes, scales)
+            nc.vector.quantize_mx(
+                out=codes[:].bitcast(FP8X4),
+                scales=scales[:],
+                in_=o2_grouped[(c, g)][:].rearrange("q n t -> q (n t)"),
+            )
+
         sums = {}
 
-        patches[0] = regroup_patches(0)
-        quantise_patches(0, patches[0])
-        spread_bias1()
-        for tile_index in range(1, REGROUP_AHEAD):
-            patches[tile_index] = regroup_patches(tile_index)
-        for tile_index in range(1, QUANTISE_AHEAD):
-            quantise_patches(tile_index, patches[tile_index])
+        def second_layer(c, g):
+            codes, scales = o2_quantised[(c, g)]
+            for e in range(REPEAT):
+                if g == 0:
+                    o3 = psum.tile([P, BANK], F32, tag="o3", bufs=2)
+                    sums[(c, e)] = o3
+                nc.tensor.matmul_mx(
+                    out=sums[(c, e)][:, : CHUNKS[c]],
+                    lhsT=w2_codes[:, g, e, :].bitcast(FP8X4),
+                    lhsT_scale=w2_scales[:, g, e, :],
+                    rhs=codes[:].bitcast(FP8X4),
+                    rhs_scale=scales[:],
+                    start=(g == 0),
+                    stop=(g == HALVES - 1),
+                )
 
-        for slot in range(SLOTS):
-            if slot < TOKEN_TILES:
-                halves[slot] = first_layer(slot)
-            if slot + QUANTISE_AHEAD < TOKEN_TILES:
-                quantise_patches(slot + QUANTISE_AHEAD, patches[slot + QUANTISE_AHEAD])
-            due = part_due(slot, QUANTISE_O2_SLOTS)
-            if due is not None:
-                o2_quantised[due] = quantise_o2(o2_grouped[due[0]][due[1]])
-            due = part_due(slot, FINISH_SLOTS)
-            if due is not None:
-                finish(due[0], due[1], sums[due], shortcuts[due])
+        pooled_banks = {}
 
-            due = part_due(slot, ADD_BIAS2_SLOTS)
-            if due is not None:
-                shortcuts[due] = add_bias2(due[1], pooled[due])
-            before = slot - ACTIVATE_LAG
-            if 0 <= before < TOKEN_TILES:
-                r = before // TILES_PER_ROUND
-                if before % TILES_PER_ROUND == 0:
-                    o2_grouped[r] = [
-                        work.tile([P, ROUND, PACK], BF16, name="o2_grouped_%d" % g, align_bytes=64)
-                        for g in range(HIDDEN_PASSES)
-                    ]
-                activate(before, halves[before], o2_grouped[r])
-            if slot + REGROUP_AHEAD < TOKEN_TILES:
-                patches[slot + REGROUP_AHEAD] = regroup_patches(slot + REGROUP_AHEAD)
+        def pool(c):
+            first, count = starts[c], CHUNKS[c]
+            four = psum.tile([P, BANK], F32, tag="pooled", bufs=1)
+            pooled_banks[c] = four
+            image = x_rows[:, PACK * first : PACK * (first + count)].rearrange(
+                "c (i u j v) -> c i u j v", u=2, j=PATCH_COLS, v=2
+            )
+            for k in range(PACK):
+                nc.tensor.matmul(
+                    out=four[:, :count].rearrange("c (i j) -> c i j", j=PATCH_COLS),
+                    lhsT=identity[:],
+                    rhs=image[:, :, k // 2, :, k % 2],
+                    start=(k == 0),
+                    stop=(k == PACK - 1),
+                )
 
-            due = part_due(slot, POOL_SLOTS)
-            if due is not None:
-                pooled[due] = pool(due[0], due[1])
-            due = part_due(slot, SECOND_LAYER_SLOTS)
-            if due is not None:
-                sums[due] = second_layer(due[1], [o2_quantised[(due[0], g)] for g in range(HIDDEN_PASSES)])
+        means = {}
+
+        def take_mean(c):
+            mean = work.tile([P, CHUNKS[c]], F32, tag="mean", bufs=2)
+            means[c] = mean
+            nc.scalar.activation(out=mean[:], in_=pooled_banks[c][:, : CHUNKS[c]], func=IDENTITY, scale=0.25)
+
+        results = {}
+
+        def finish(c, e):
+            count = CHUNKS[c]
+            if e == 0:
+                result = work.tile([P, REPEAT, count], F32, tag="result", bufs=2)
+                results[c] = result
+            nc.vector.scalar_tensor_tensor(
+                out=results[c][:, e, :],
+                in0=sums[(c, e)][:, :count],
+                scalar=bias2_col[:, e : e + 1],
+                in1=means[c][:],
+                op0=ADD,
+                op1=ADD,
+            )
+            for b, s, offset, take in image_parts(c):
+                nc.sync.dma_start(
+                    out=out[b].rearrange("(c e) i j -> c e (i j)", e=REPEAT)[:, e, s : s + take],
+                    in_=results[c][:, e, offset : offset + take],
+                )
+
+        tiles = [(c, g, t) for c in range(n_chunks) for g in range(HALVES) for t in range(PACK)]
+
+        def tensor_step(index):
+            c, g, t = tiles[index]
+            first_layer(c, g, t)
+            if t == PACK - 1 and g == 0:
+                pool(c)
+                if c >= 1:
+                    second_layer(c - 1, 0)
+            if t == PACK - 1 and g == 1 and c >= 1:
+                second_layer(c - 1, 1)
+
+        regroup(0)
+        sort_w1_scales(0)
+        quantise_patches(0)
+        sort_w1_codes(0)
+        sort_w1_scales(1)
+        sort_w1_codes(1)
+        regroup(1)
+        quantise_patches(1)
+        for index in range(LEAD):
+            tensor_step(index)
+
+        for index in range(len(tiles)):
+            c, g, t = tiles[index]
+            silu(c, g, t)
+            if index + LEAD < len(tiles):
+                tensor_step(index + LEAD)
+            if t < PACK - 1:
+                continue
+            last = c == n_chunks - 1
+            interleave(c, g)
+            if g == 0:
+                take_mean(c)
+                if c == 0:
+                    sort_w2_codes()
+                else:
+                    finish(c - 1, 0)
+                quantise_o2(c, g)
+                if c == 0:
+                    sort_w2_scales()
+                else:
+                    finish(c - 1, 1)
+            else:
+                if c + 2 < n_chunks:
+                    regroup(c + 2)
+                quantise_o2(c, g)
+                if c + 2 < n_chunks:
+                    quantise_patches(c + 2)
+            if last:
+                second_layer(c, g)
+        finish(n_chunks - 1, 0)
+        finish(n_chunks - 1, 1)

@@ -99,19 +99,17 @@ def tile_memoryefficientpatchdownscale_kernel(
                 out=w1_codes_raw[:, g * BANK : (g + 1) * BANK], in_=w1_bytes[:, g * BANK : (g + 1) * BANK]
             )
         load_x(1)
-        load_x(2)
+        nc.sync.dma_start(
+            out=w2_codes_raw[:], in_=weight2_words.rearrange("g p n t -> p g (n t)").bitcast(I32)
+        )
         for quadrant in range(4):
             nc.sync.dma_start(
                 out=w2_scales_raw[32 * quadrant : 32 * quadrant + 4, :, :].bitcast(I32),
                 in_=weight2_scales[:, 4 * quadrant : 4 * quadrant + 4, :].rearrange("g r n -> r g n").bitcast(I32),
             )
-        for g in range(HALVES):
-            nc.sync.dma_start(
-                out=w2_codes_raw[:, g, :], in_=weight2_words[g].rearrange("p n t -> p (n t)").bitcast(I32)
-            )
         with nc.allow_non_contiguous_dma(reason="bias values, four or two to a partition"):
             nc.sync.dma_start(out=bias2_col[:], in_=bias2.rearrange("(c e) -> c e", e=REPEAT))
-        for c in range(3, n_chunks):
+        for c in range(2, n_chunks):
             load_x(c)
 
         identity = keep.tile([P, P], BF16)

@@ -198,7 +198,10 @@ def tile_memoryefficientpatchdownscale_kernel(
         def interleave(c, g):
             grouped = work.tile([P, CHUNKS[c], PACK], BF16, tag="o2_grouped", bufs=2, align_bytes=64)
             o2_grouped[(c, g)] = grouped
-            nc.vector.tensor_copy(out=grouped[:], in_=o2_rows[(c, g)][:].rearrange("q t n -> q n t"))
+            nc.vector.tensor_copy(
+                out=grouped[:].rearrange("q (b i) t -> q b t i", i=4),
+                in_=o2_rows[(c, g)][:].rearrange("q t (b i) -> q b t i", i=4),
+            )
 
         o2_quantised = {}
 

@@ -117,8 +117,8 @@ def tile_memoryefficientpatchdownscale_kernel(
 
         def sort_w1_scales(g):
             nc.vector.tensor_copy(
-                out=w1_scales[:, g].rearrange("q t m -> q m t"),
-                in_=w1_scales_raw[:, g * BANK : (g + 1) * BANK].rearrange("q (m t) -> q m t", t=PACK),
+                out=w1_scales[:, g],
+                in_=w1_scales_raw[:, g * BANK : (g + 1) * BANK].rearrange("q (m t) -> q t m", t=PACK),
             )
 
         def sort_w1_codes(g):
@@ -134,8 +134,8 @@ def tile_memoryefficientpatchdownscale_kernel(
 
         def sort_w2_scales():
             nc.vector.tensor_copy(
-                out=w2_scales[:].rearrange("q g e c -> q g c e"),
-                in_=w2_scales_raw[:].rearrange("q g (c e) -> q g c e", e=REPEAT),
+                out=w2_scales[:],
+                in_=w2_scales_raw[:].rearrange("q g (c e) -> q g e c", e=REPEAT),
             )
 
         patches = {}

@@ -29,7 +29,14 @@ FLOPS = 2 * TOKENS * (CHANNELS * PACK) * HIDDEN + 2 * TOKENS * HIDDEN * OUT_CHAN
 
 CHUNKS = (256, 512, 512, 512, 256)
 LEAD = 5
-REGROUP_ON_SCALAR = (0,)
+SPLIT = (0, 1, 2, 3, 4,)
+PREPS = ((0,), (1,), (2,), (3,), (4,))
+SCALAR_SHARE = (256, 0, 0, 0, 0)
+FAST_INTERLEAVE = True
+ROWS_BUFS = 3
+RUN = 4
+MEAN_BUFS = 3
+SECOND_LAYER_BEHIND = (5, 7)
 
 
 def tile_memoryefficientpatchdownscale_kernel(
@@ -39,16 +46,19 @@ def tile_memoryefficientpatchdownscale_kernel(
     starts = [sum(CHUNKS[:c]) for c in range(len(CHUNKS))]
     n_chunks = len(CHUNKS)
 
-    def image_parts(c):
+    def image_parts(first, count):
         parts = []
-        first, count = starts[c], CHUNKS[c]
+        offset = 0
         while count > 0:
-            b, s = divmod(first, TOKENS_PER_IMAGE)
+            b, s = divmod(first + offset, TOKENS_PER_IMAGE)
             take = min(count, TOKENS_PER_IMAGE - s)
-            parts.append((b, s, first - starts[c], take))
-            first += take
+            parts.append((b, s, offset, take))
+            offset += take
             count -= take
         return parts
+
+    def unit_of(c, g):
+        return (c, (g,)) if c in SPLIT else (c, tuple(range(HALVES)))
 
     with ExitStack() as ctx:
         keep = ctx.enter_context(tc.tile_pool(name="keep", bufs=1))
@@ -78,7 +88,7 @@ def tile_memoryefficientpatchdownscale_kernel(
         p_scales = keep.tile([P, TOKENS], U8, align_bytes=64)
 
         def load_x(c):
-            for b, s, offset, count in image_parts(c):
+            for b, s, offset, count in image_parts(starts[c], CHUNKS[c]):
                 first = starts[c] + offset
                 nc.sync.dma_start(
                     out=x_rows[:, PACK * first : PACK * (first + count)],
@@ -140,27 +150,30 @@ def tile_memoryefficientpatchdownscale_kernel(
 
         patches = {}
 
-        def regroup(c):
-            first, count = starts[c], CHUNKS[c]
+        def regroup(k):
+            first = starts[PREPS[k][0]]
+            count = sum(CHUNKS[c] for c in PREPS[k])
             grouped = work.tile([P, PACK * count], BF16, tag="patches", bufs=2, align_bytes=64)
-            patches[c] = grouped
+            patches[k] = grouped
             dst = grouped[:].bitcast(F32).rearrange("c (i j u) -> c i j u", j=PATCH_COLS, u=2)
             src = (
                 x_rows[:, PACK * first : PACK * (first + count)]
                 .bitcast(F32)
                 .rearrange("c (i u j) -> c i j u", u=2, j=PATCH_COLS)
             )
-            if c in REGROUP_ON_SCALAR:
-                nc.scalar.copy(out=dst, in_=src)
-            else:
-                nc.vector.tensor_copy(out=dst, in_=src)
+            rows = SCALAR_SHARE[k] // PATCH_COLS
+            if rows > 0:
+                nc.scalar.copy(out=dst[:, :rows], in_=src[:, :rows])
+            if rows < count // PATCH_COLS:
+                nc.vector.tensor_copy(out=dst[:, rows:], in_=src[:, rows:])
 
-        def quantise_patches(c):
-            first, count = starts[c], CHUNKS[c]
+        def quantise_patches(k):
+            first = starts[PREPS[k][0]]
+            count = sum(CHUNKS[c] for c in PREPS[k])
             nc.vector.quantize_mx(
                 out=p_codes[:, first : first + count].bitcast(FP8X4),
                 scales=p_scales[:, first : first + count],
-                in_=patches[c][:],
+                in_=patches[k][:],
             )
 
         o1_banks = {}
@@ -183,11 +196,13 @@ def tile_memoryefficientpatchdownscale_kernel(
 
         def silu(c, g, t):
             count = CHUNKS[c]
-            if t == 0:
-                rows = work.tile([P, PACK, count], BF16, tag="o2_rows", bufs=3)
-                o2_rows[(c, g)] = rows
+            unit = unit_of(c, g)
+            if g == unit[1][0] and t == 0:
+                rows = work.tile([P, PACK, len(unit[1]) * count], BF16, tag="o2_rows", bufs=ROWS_BUFS)
+                o2_rows[unit] = rows
+            place = (g - unit[1][0]) * count
             nc.scalar.activation(
-                out=o2_rows[(c, g)][:, t, :],
+                out=o2_rows[unit][:, t, place : place + count],
                 in_=o1_banks[(c, g, t)][:, :count],
                 func=SILU,
                 bias=bias1_col[:, g, t : t + 1],
@@ -195,43 +210,62 @@ def tile_memoryefficientpatchdownscale_kernel(
 
         o2_grouped = {}
 
-        def interleave(c, g):
-            grouped = work.tile([P, CHUNKS[c], PACK], BF16, tag="o2_grouped", bufs=2, align_bytes=64)
-            o2_grouped[(c, g)] = grouped
-            nc.vector.tensor_copy(
-                out=grouped[:].rearrange("q (b i) t -> q b t i", i=4),
-                in_=o2_rows[(c, g)][:].rearrange("q t (b i) -> q b t i", i=4),
-            )
+        def interleave(unit):
+            columns = len(unit[1]) * CHUNKS[unit[0]]
+            grouped = work.tile([P, columns, PACK], BF16, tag="o2_grouped", bufs=2, align_bytes=64)
+            o2_grouped[unit] = grouped
+            if FAST_INTERLEAVE:
+                nc.vector.tensor_copy(
+                    out=grouped[:].rearrange("q (b i) t -> q b t i", i=RUN),
+                    in_=o2_rows[unit][:].rearrange("q t (b i) -> q b t i", i=RUN),
+                )
+            else:
+                nc.vector.tensor_copy(out=grouped[:], in_=o2_rows[unit][:].rearrange("q t n -> q n t"))
 
         o2_quantised = {}
 
-        def quantise_o2(c, g):
-            codes = work.tile([P, CHUNKS[c]], U32, tag="o2_codes", bufs=4, align_bytes=64)
-            scales = work.tile([P, CHUNKS[c]], U8, tag="o2_scales", bufs=4, align_bytes=64)
-            o2_quantised[(c, g)] = (codes, scales)
+        def quantise_o2(unit):
+            columns = len(unit[1]) * CHUNKS[unit[0]]
+            codes = work.tile([P, columns], U32, tag="o2_codes", bufs=3, align_bytes=64)
+            scales = work.tile([P, columns], U8, tag="o2_scales", bufs=3, align_bytes=64)
+            o2_quantised[unit] = (codes, scales)
             nc.vector.quantize_mx(
                 out=codes[:].bitcast(FP8X4),
                 scales=scales[:],
-                in_=o2_grouped[(c, g)][:].rearrange("q n t -> q (n t)"),
+                in_=o2_grouped[unit][:].rearrange("q n t -> q (n t)"),
             )
 
         sums = {}
 
-        def second_layer(c, g):
-            codes, scales = o2_quantised[(c, g)]
-            for e in range(REPEAT):
-                if g == 0:
+        def second_layer_pass(c, g, e):
+            count = CHUNKS[c]
+            unit = unit_of(c, g)
+            codes, scales = o2_quantised[unit]
+            place = (g - unit[1][0]) * count
+            if g == 0:
+                if c == n_chunks - 1:
+                    o3 = psum.tile([P, BANK], F32, tag="o1", bufs=LEAD)
+                else:
                     o3 = psum.tile([P, BANK], F32, tag="o3", bufs=2)
-                    sums[(c, e)] = o3
-                nc.tensor.matmul_mx(
-                    out=sums[(c, e)][:, : CHUNKS[c]],
-                    lhsT=w2_codes[:, g, e, :].bitcast(FP8X4),
-                    lhsT_scale=w2_scales[:, g, e, :],
-                    rhs=codes[:].bitcast(FP8X4),
-                    rhs_scale=scales[:],
-                    start=(g == 0),
-                    stop=(g == HALVES - 1),
-                )
+                sums[(c, e)] = o3
+            nc.tensor.matmul_mx(
+                out=sums[(c, e)][:, :count],
+                lhsT=w2_codes[:, g, e, :].bitcast(FP8X4),
+                lhsT_scale=w2_scales[:, g, e, :],
+                rhs=codes[:, place : place + count].bitcast(FP8X4),
+                rhs_scale=scales[:, place : place + count],
+                start=(g == 0),
+                stop=(g == HALVES - 1),
+            )
+
+        def second_layer(c, halves):
+            if len(halves) == HALVES:
+                for e in range(REPEAT):
+                    for g in halves:
+                        second_layer_pass(c, g, e)
+            else:
+                for e in range(REPEAT):
+                    second_layer_pass(c, halves[0], e)
 
         pooled_banks = {}
 
@@ -254,7 +288,7 @@ def tile_memoryefficientpatchdownscale_kernel(
         means = {}
 
         def take_mean(c):
-            mean = work.tile([P, CHUNKS[c]], F32, tag="mean", bufs=2)
+            mean = work.tile([P, CHUNKS[c]], F32, tag="mean", bufs=MEAN_BUFS)
             means[c] = mean
             nc.scalar.activation(out=mean[:], in_=pooled_banks[c][:, : CHUNKS[c]], func=IDENTITY, scale=0.25)
 
@@ -273,7 +307,7 @@ def tile_memoryefficientpatchdownscale_kernel(
                 op0=ADD,
                 op1=ADD,
             )
-            for b, s, offset, take in image_parts(c):
+            for b, s, offset, take in image_parts(starts[c], count):
                 nc.sync.dma_start(
                     out=out[b].rearrange("(c e) i j -> c e (i j)", e=REPEAT)[:, e, s : s + take],
                     in_=results[c][:, e, offset : offset + take],
@@ -284,12 +318,20 @@ def tile_memoryefficientpatchdownscale_kernel(
         def tensor_step(index):
             c, g, t = tiles[index]
             first_layer(c, g, t)
-            if t == PACK - 1 and g == 0:
+            for before in range(n_chunks - 1):
+                for half in range(HALVES):
+                    if index == HALVES * PACK * (before + 1) + SECOND_LAYER_BEHIND[half]:
+                        second_layer(before, (half,))
+            if t < PACK - 1:
+                return
+            if g == 0:
                 pool(c)
-                if c >= 1:
-                    second_layer(c - 1, 0)
-            if t == PACK - 1 and g == 1 and c >= 1:
-                second_layer(c - 1, 1)
+
+        def prep_due(c):
+            for k in range(len(PREPS)):
+                if PREPS[k][0] == c + 2:
+                    return k
+            return None
 
         regroup(0)
         sort_w1_scales(0)
@@ -309,26 +351,37 @@ def tile_memoryefficientpatchdownscale_kernel(
                 tensor_step(index + LEAD)
             if t < PACK - 1:
                 continue
-            last = c == n_chunks - 1
-            interleave(c, g)
             if g == 0:
                 take_mean(c)
-                if c == 0:
+            unit = unit_of(c, g)
+            if g != unit[1][-1]:
+                continue
+            last = c == n_chunks - 1
+            k = prep_due(c)
+            if last:
+                if g == 0:
+                    interleave(unit)
+                    continue
+                interleave(unit)
+                for half in range(HALVES):
+                    quantise_o2(unit_of(c, half))
+                    second_layer(c, (half,))
+                for e in range(REPEAT):
+                    finish(c - 1, e)
+                continue
+            interleave(unit)
+            if c == 0:
+                if g == 0:
                     sort_w2_codes()
                 else:
-                    finish(c - 1, 0)
-                quantise_o2(c, g)
-                if c == 0:
                     sort_w2_scales()
-                else:
-                    finish(c - 1, 1)
             else:
-                if c + 2 < n_chunks:
-                    regroup(c + 2)
-                quantise_o2(c, g)
-                if c + 2 < n_chunks:
-                    quantise_patches(c + 2)
-            if last:
-                second_layer(c, g)
+                finish(c - 1, g)
+            quantise_o2(unit)
+            if k is not None:
+                if g == 0:
+                    regroup(k)
+                else:
+                    quantise_patches(k)
         finish(n_chunks - 1, 0)
         finish(n_chunks - 1, 1)

@@ -36,7 +36,7 @@ FAST_INTERLEAVE = True
 ROWS_BUFS = 3
 RUN = 4
 MEAN_BUFS = 3
-SECOND_LAYER_BEHIND = (5, 7)
+SECOND_LAYER_BEHIND = (7, 7)
 
 
 def tile_memoryefficientpatchdownscale_kernel(
@@ -210,11 +210,13 @@ def tile_memoryefficientpatchdownscale_kernel(
 
         o2_grouped = {}
 
-        def interleave(unit):
+        def interleave(unit, on_scalar=False):
             columns = len(unit[1]) * CHUNKS[unit[0]]
-            grouped = work.tile([P, columns, PACK], BF16, tag="o2_grouped", bufs=2, align_bytes=64)
+            grouped = work.tile([P, columns, PACK], BF16, tag="o2_grouped", bufs=3, align_bytes=64)
             o2_grouped[unit] = grouped
-            if FAST_INTERLEAVE:
+            if on_scalar:
+                nc.scalar.copy(out=grouped[:], in_=o2_rows[unit][:].rearrange("q t n -> q n t"))
+            elif FAST_INTERLEAVE:
                 nc.vector.tensor_copy(
                     out=grouped[:].rearrange("q (b i) t -> q b t i", i=RUN),
                     in_=o2_rows[unit][:].rearrange("q t (b i) -> q b t i", i=RUN),
@@ -361,13 +363,13 @@ def tile_memoryefficientpatchdownscale_kernel(
             if last:
                 if g == 0:
                     interleave(unit)
+                    finish(c - 1, 0)
                     continue
-                interleave(unit)
+                interleave(unit, on_scalar=True)
                 for half in range(HALVES):
                     quantise_o2(unit_of(c, half))
                     second_layer(c, (half,))
-                for e in range(REPEAT):
-                    finish(c - 1, e)
+                finish(c - 1, 1)
                 continue
             interleave(unit)
             if c == 0:

@@ -73,7 +73,7 @@ def tile_memoryefficientpatchdownscale_kernel(
 
         w1_scales_raw = keep.tile([P, HIDDEN], U8, align_bytes=64)
         w2_scales_raw = keep.tile([P, HALVES, OUT_CHANNELS], U8, align_bytes=64)
-        nc.vector.memset(w1_scales_raw[:].bitcast(I32), 0)
+        nc.gpsimd.memset(w1_scales_raw[:].bitcast(F32), 0.0)
         nc.vector.memset(w2_scales_raw[:].rearrange("q g n -> q (g n)").bitcast(I32), 0)
         w1_codes_raw = keep.tile([P, HIDDEN], I32, align_bytes=64)
         w2_codes_raw = keep.tile([P, HALVES, OUT_CHANNELS], I32, align_bytes=64)
@@ -135,6 +135,16 @@ def tile_memoryefficientpatchdownscale_kernel(
             nc.vector.tensor_copy(
                 out=w1_codes[:, g],
                 in_=w1_codes_raw[:, g * BANK : (g + 1) * BANK].rearrange("p (m t) -> p t m", t=PACK),
+            )
+
+        def sort_w1_tile(g, t):
+            nc.vector.tensor_copy(
+                out=w1_scales[:, g, t, :],
+                in_=w1_scales_raw[:, g * BANK : (g + 1) * BANK].rearrange("q (m t) -> q t m", t=PACK)[:, t, :],
+            )
+            nc.vector.tensor_copy(
+                out=w1_codes[:, g, t, :],
+                in_=w1_codes_raw[:, g * BANK : (g + 1) * BANK].rearrange("p (m t) -> p t m", t=PACK)[:, t, :],
             )
 
         def sort_w2_codes():
@@ -336,9 +346,9 @@ def tile_memoryefficientpatchdownscale_kernel(
             return None
 
         regroup(0)
-        sort_w1_scales(0)
         quantise_patches(0)
-        sort_w1_codes(0)
+        for t in range(PACK):
+            sort_w1_tile(0, t)
         sort_w1_scales(1)
         sort_w1_codes(1)
         regroup(1)

@@ -336,7 +336,7 @@ def tile_memoryefficientpatchdownscale_kernel(
                         second_layer(before, (half,))
             if t < PACK - 1:
                 return
-            if g == 0:
+            if g == 0 and c > 0:
                 pool(c)
 
         def prep_due(c):
@@ -353,6 +353,8 @@ def tile_memoryefficientpatchdownscale_kernel(
         sort_w1_codes(1)
         regroup(1)
         quantise_patches(1)
+        pool(0)
+        take_mean(0)
         for index in range(LEAD):
             tensor_step(index)
 
@@ -363,7 +365,7 @@ def tile_memoryefficientpatchdownscale_kernel(
                 tensor_step(index + LEAD)
             if t < PACK - 1:
                 continue
-            if g == 0:
+            if g == 0 and c > 0:
                 take_mean(c)
             unit = unit_of(c, g)
             if g != unit[1][-1]:

@@ -108,7 +108,8 @@ def tile_memoryefficientpatchdownscale_kernel(
             nc.sync.dma_start(
                 out=w1_codes_raw[:, g * BANK : (g + 1) * BANK], in_=w1_bytes[:, g * BANK : (g + 1) * BANK]
             )
-        load_x(1)
+            if g == 0:
+                load_x(1)
         nc.sync.dma_start(
             out=w2_codes_raw[:], in_=weight2_words.rearrange("g p n t -> p g (n t)").bitcast(I32)
         )
@@ -137,11 +138,13 @@ def tile_memoryefficientpatchdownscale_kernel(
                 in_=w1_codes_raw[:, g * BANK : (g + 1) * BANK].rearrange("p (m t) -> p t m", t=PACK),
             )
 
-        def sort_w1_tile(g, t):
+        def sort_w1_tile_scales(g, t):
             nc.vector.tensor_copy(
                 out=w1_scales[:, g, t, :],
                 in_=w1_scales_raw[:, g * BANK : (g + 1) * BANK].rearrange("q (m t) -> q t m", t=PACK)[:, t, :],
             )
+
+        def sort_w1_tile_codes(g, t):
             nc.vector.tensor_copy(
                 out=w1_codes[:, g, t, :],
                 in_=w1_codes_raw[:, g * BANK : (g + 1) * BANK].rearrange("p (m t) -> p t m", t=PACK)[:, t, :],
@@ -346,12 +349,17 @@ def tile_memoryefficientpatchdownscale_kernel(
             return None
 
         regroup(0)
+        sort_w1_tile_scales(0, 0)
+        sort_w1_tile_scales(0, 1)
         quantise_patches(0)
-        for t in range(PACK):
-            sort_w1_tile(0, t)
+        sort_w1_tile_codes(0, 0)
+        sort_w1_tile_codes(0, 1)
+        for t in range(2, PACK):
+            sort_w1_tile_scales(0, t)
+            sort_w1_tile_codes(0, t)
         sort_w1_scales(1)
-        sort_w1_codes(1)
         regroup(1)
+        sort_w1_codes(1)
         quantise_patches(1)
         pool(0)
         take_mean(0)

from contextlib import ExitStack

import concourse.mybir as mybir
from concourse.masks import make_identity

F32 = mybir.dt.float32
BF16 = mybir.dt.bfloat16
I32 = mybir.dt.int32
U32 = mybir.dt.uint32
U8 = mybir.dt.uint8
FP8X4 = mybir.dt.float8_e4m3fn_x4
ADD = mybir.AluOpType.add
SILU = mybir.ActivationFunctionType.Silu
IDENTITY = mybir.ActivationFunctionType.Identity

P = 128
PACK = 4
BANK = 512

BATCH, CHANNELS, HEIGHT, WIDTH = 2, 128, 64, 64
HIDDEN, OUT_CHANNELS = 1024, 256
PATCH_COLS = WIDTH // 2
TOKENS_PER_IMAGE = (HEIGHT // 2) * PATCH_COLS
TOKENS = BATCH * TOKENS_PER_IMAGE
HALVES = HIDDEN // (P * PACK)
REPEAT = OUT_CHANNELS // CHANNELS

FLOPS = 2 * TOKENS * (CHANNELS * PACK) * HIDDEN + 2 * TOKENS * HIDDEN * OUT_CHANNELS

CHUNKS = (256, 512, 512, 512, 256)
LEAD = 5
SPLIT = (0, 1, 2, 3, 4,)
PREPS = ((0,), (1,), (2,), (3,), (4,))
SCALAR_SHARE = (256, 0, 0, 0, 0)
FAST_INTERLEAVE = True
ROWS_BUFS = 3
RUN = 4
MEAN_BUFS = 3
SECOND_LAYER_BEHIND = (7, 7)


def tile_memoryefficientpatchdownscale_kernel(
    tc, x, weight1_words, weight1_scales, bias1, weight2_words, weight2_scales, bias2, out
):
    nc = tc.nc
    starts = [sum(CHUNKS[:c]) for c in range(len(CHUNKS))]
    n_chunks = len(CHUNKS)

    def image_parts(first, count):
        parts = []
        offset = 0
        while count > 0:
            b, s = divmod(first + offset, TOKENS_PER_IMAGE)
            take = min(count, TOKENS_PER_IMAGE - s)
            parts.append((b, s, offset, take))
            offset += take
            count -= take
        return parts

    def unit_of(c, g):
        return (c, (g,)) if c in SPLIT else (c, tuple(range(HALVES)))

    with ExitStack() as ctx:
        keep = ctx.enter_context(tc.tile_pool(name="keep", bufs=1))
        work = ctx.enter_context(tc.tile_pool(name="work", bufs=2))
        psum = ctx.enter_context(tc.psum_pool(name="psum", bufs=2))
        ctx.enter_context(tc.manual_schedule())

        table_in = keep.tile([P, 1], F32)
        table_out = keep.tile([P, 1], F32)
        nc.vector.memset(table_in[:], 0.0)
        nc.scalar.activation(out=table_out[:], in_=table_in[:], func=SILU)

        w1_scales_raw = keep.tile([P, HIDDEN], U8, align_bytes=64)
        w2_scales_raw = keep.tile([P, HALVES, OUT_CHANNELS], U8, align_bytes=64)
        nc.gpsimd.memset(w1_scales_raw[:].bitcast(F32), 0.0)
        nc.vector.memset(w2_scales_raw[:].rearrange("q g n -> q (g n)").bitcast(I32), 0)
        w1_codes_raw = keep.tile([P, HIDDEN], I32, align_bytes=64)
        w2_codes_raw = keep.tile([P, HALVES, OUT_CHANNELS], I32, align_bytes=64)
        w1_codes = keep.tile([P, HALVES, PACK, P], I32, align_bytes=64)
        w1_scales = keep.tile([P, HALVES, PACK, P], U8, align_bytes=64)
        w2_codes = keep.tile([P, HALVES, REPEAT, P], I32, align_bytes=64)
        w2_scales = keep.tile([P, HALVES, REPEAT, P], U8, align_bytes=64)
        bias1_col = keep.tile([P, HALVES, PACK], BF16)
        bias2_col = keep.tile([P, REPEAT], BF16)
        x_rows = keep.tile([P, BATCH * HEIGHT * WIDTH], BF16)
        p_codes = keep.tile([P, TOKENS], U32, align_bytes=64)
        p_scales = keep.tile([P, TOKENS], U8, align_bytes=64)

        def load_x(c):
            for b, s, offset, count in image_parts(starts[c], CHUNKS[c]):
                first = starts[c] + offset
                nc.sync.dma_start(
                    out=x_rows[:, PACK * first : PACK * (first + count)],
                    in_=x[b].rearrange("c h w -> c (h w)")[:, PACK * s : PACK * (s + count)],
                )

        load_x(0)
        with nc.allow_non_contiguous_dma(reason="bias values, four or two to a partition"):
            nc.sync.dma_start(out=bias1_col[:], in_=bias1.rearrange("(g q t) -> q g t", g=HALVES, t=PACK))
        for quadrant in range(4):
            nc.sync.dma_start(
                out=w1_scales_raw[32 * quadrant : 32 * quadrant + 4, :].bitcast(I32),
                in_=weight1_scales[0, 4 * quadrant : 4 * quadrant + 4, :].bitcast(I32),
            )
        w1_bytes = weight1_words[0].rearrange("p n t -> p (n t)").bitcast(I32)
        for g in range(HALVES):
            nc.sync.dma_start(
                out=w1_codes_raw[:, g * BANK : (g + 1) * BANK], in_=w1_bytes[:, g * BANK : (g + 1) * BANK]
            )
            if g == 0:
                load_x(1)
        nc.sync.dma_start(
            out=w2_codes_raw[:], in_=weight2_words.rearrange("g p n t -> p g (n t)").bitcast(I32)
        )
        for quadrant in range(4):
            nc.sync.dma_start(
                out=w2_scales_raw[32 * quadrant : 32 * quadrant + 4, :, :].bitcast(I32),
                in_=weight2_scales[:, 4 * quadrant : 4 * quadrant + 4, :].rearrange("g r n -> r g n").bitcast(I32),
            )
        with nc.allow_non_contiguous_dma(reason="bias values, four or two to a partition"):
            nc.sync.dma_start(out=bias2_col[:], in_=bias2.rearrange("(c e) -> c e", e=REPEAT))
        for c in range(2, n_chunks):
            load_x(c)

        identity = keep.tile([P, P], BF16)
        make_identity(nc, identity[:])

        def sort_w1_scales(g):
            nc.vector.tensor_copy(
                out=w1_scales[:, g],
                in_=w1_scales_raw[:, g * BANK : (g + 1) * BANK].rearrange("q (m t) -> q t m", t=PACK),
            )

        def sort_w1_codes(g):
            nc.vector.tensor_copy(
                out=w1_codes[:, g],
                in_=w1_codes_raw[:, g * BANK : (g + 1) * BANK].rearrange("p (m t) -> p t m", t=PACK),
            )

        def sort_w1_tile_scales(g, t):
            nc.vector.tensor_copy(
                out=w1_scales[:, g, t, :],
                in_=w1_scales_raw[:, g * BANK : (g + 1) * BANK].rearrange("q (m t) -> q t m", t=PACK)[:, t, :],
            )

        def sort_w1_tile_codes(g, t):
            nc.vector.tensor_copy(
                out=w1_codes[:, g, t, :],
                in_=w1_codes_raw[:, g * BANK : (g + 1) * BANK].rearrange("p (m t) -> p t m", t=PACK)[:, t, :],
            )

        def sort_w2_codes():
            nc.vector.tensor_copy(
                out=w2_codes[:], in_=w2_codes_raw[:].rearrange("p g (c e) -> p g e c", e=REPEAT)
            )

        def sort_w2_scales():
            nc.vector.tensor_copy(
                out=w2_scales[:],
                in_=w2_scales_raw[:].rearrange("q g (c e) -> q g e c", e=REPEAT),
            )

        patches = {}

        def regroup(k):
            first = starts[PREPS[k][0]]
            count = sum(CHUNKS[c] for c in PREPS[k])
            grouped = work.tile([P, PACK * count], BF16, tag="patches", bufs=2, align_bytes=64)
            patches[k] = grouped
            dst = grouped[:].bitcast(F32).rearrange("c (i j u) -> c i j u", j=PATCH_COLS, u=2)
            src = (
                x_rows[:, PACK * first : PACK * (first + count)]
                .bitcast(F32)
                .rearrange("c (i u j) -> c i j u", u=2, j=PATCH_COLS)
            )
            rows = SCALAR_SHARE[k] // PATCH_COLS
            if rows > 0:
                nc.scalar.copy(out=dst[:, :rows], in_=src[:, :rows])
            if rows < count // PATCH_COLS:
                nc.vector.tensor_copy(out=dst[:, rows:], in_=src[:, rows:])

        def quantise_patches(k):
            first = starts[PREPS[k][0]]
            count = sum(CHUNKS[c] for c in PREPS[k])
            nc.vector.quantize_mx(
                out=p_codes[:, first : first + count].bitcast(FP8X4),
                scales=p_scales[:, first : first + count],
                in_=patches[k][:],
            )

        o1_banks = {}

        def first_layer(c, g, t):
            first, count = starts[c], CHUNKS[c]
            o1 = psum.tile([P, BANK], F32, tag="o1", bufs=LEAD)
            o1_banks[(c, g, t)] = o1
            nc.tensor.matmul_mx(
                out=o1[:, :count],
                lhsT=w1_codes[:, g, t, :].bitcast(FP8X4),
                lhsT_scale=w1_scales[:, g, t, :],
                rhs=p_codes[:, first : first + count].bitcast(FP8X4),
                rhs_scale=p_scales[:, first : first + count],
                start=True,
                stop=True,
            )

        o2_rows = {}

        def silu(c, g, t):
            count = CHUNKS[c]
            unit = unit_of(c, g)
            if g == unit[1][0] and t == 0:
                rows = work.tile([P, PACK, len(unit[1]) * count], BF16, tag="o2_rows", bufs=ROWS_BUFS)
                o2_rows[unit] = rows
            place = (g - unit[1][0]) * count
            nc.scalar.activation(
                out=o2_rows[unit][:, t, place : place + count],
                in_=o1_banks[(c, g, t)][:, :count],
                func=SILU,
                bias=bias1_col[:, g, t : t + 1],
            )

        o2_grouped = {}

        def interleave(unit, on_scalar=False):
            columns = len(unit[1]) * CHUNKS[unit[0]]
            grouped = work.tile([P, columns, PACK], BF16, tag="o2_grouped", bufs=3, align_bytes=64)
            o2_grouped[unit] = grouped
            if on_scalar:
                nc.scalar.copy(out=grouped[:], in_=o2_rows[unit][:].rearrange("q t n -> q n t"))
            elif FAST_INTERLEAVE:
                nc.vector.tensor_copy(
                    out=grouped[:].rearrange("q (b i) t -> q b t i", i=RUN),
                    in_=o2_rows[unit][:].rearrange("q t (b i) -> q b t i", i=RUN),
                )
            else:
                nc.vector.tensor_copy(out=grouped[:], in_=o2_rows[unit][:].rearrange("q t n -> q n t"))

        o2_quantised = {}

        def quantise_o2(unit):
            columns = len(unit[1]) * CHUNKS[unit[0]]
            codes = work.tile([P, columns], U32, tag="o2_codes", bufs=3, align_bytes=64)
            scales = work.tile([P, columns], U8, tag="o2_scales", bufs=3, align_bytes=64)
            o2_quantised[unit] = (codes, scales)
            nc.vector.quantize_mx(
                out=codes[:].bitcast(FP8X4),
                scales=scales[:],
                in_=o2_grouped[unit][:].rearrange("q n t -> q (n t)"),
            )

        sums = {}

        def second_layer_pass(c, g, e):
            count = CHUNKS[c]
            unit = unit_of(c, g)
            codes, scales = o2_quantised[unit]
            place = (g - unit[1][0]) * count
            if g == 0:
                if c == n_chunks - 1:
                    o3 = psum.tile([P, BANK], F32, tag="o1", bufs=LEAD)
                else:
                    o3 = psum.tile([P, BANK], F32, tag="o3", bufs=2)
                sums[(c, e)] = o3
            nc.tensor.matmul_mx(
                out=sums[(c, e)][:, :count],
                lhsT=w2_codes[:, g, e, :].bitcast(FP8X4),
                lhsT_scale=w2_scales[:, g, e, :],
                rhs=codes[:, place : place + count].bitcast(FP8X4),
                rhs_scale=scales[:, place : place + count],
                start=(g == 0),
                stop=(g == HALVES - 1),
            )

        def second_layer(c, halves):
            if len(halves) == HALVES:
                for e in range(REPEAT):
                    for g in halves:
                        second_layer_pass(c, g, e)
            else:
                for e in range(REPEAT):
                    second_layer_pass(c, halves[0], e)

        pooled_banks = {}

        def pool(c):
            first, count = starts[c], CHUNKS[c]
            four = psum.tile([P, BANK], F32, tag="pooled", bufs=1)
            pooled_banks[c] = four
            image = x_rows[:, PACK * first : PACK * (first + count)].rearrange(
                "c (i u j v) -> c i u j v", u=2, j=PATCH_COLS, v=2
            )
            for k in range(PACK):
                nc.tensor.matmul(
                    out=four[:, :count].rearrange("c (i j) -> c i j", j=PATCH_COLS),
                    lhsT=identity[:],
                    rhs=image[:, :, k // 2, :, k % 2],
                    start=(k == 0),
                    stop=(k == PACK - 1),
                )

        means = {}

        def take_mean(c):
            mean = work.tile([P, CHUNKS[c]], F32, tag="mean", bufs=MEAN_BUFS)
            means[c] = mean
            nc.scalar.activation(out=mean[:], in_=pooled_banks[c][:, : CHUNKS[c]], func=IDENTITY, scale=0.25)

        results = {}

        def finish(c, e):
            count = CHUNKS[c]
            if e == 0:
                result = work.tile([P, REPEAT, count], F32, tag="result", bufs=2)
                results[c] = result
            nc.vector.scalar_tensor_tensor(
                out=results[c][:, e, :],
                in0=sums[(c, e)][:, :count],
                scalar=bias2_col[:, e : e + 1],
                in1=means[c][:],
                op0=ADD,
                op1=ADD,
            )
            for b, s, offset, take in image_parts(starts[c], count):
                nc.sync.dma_start(
                    out=out[b].rearrange("(c e) i j -> c e (i j)", e=REPEAT)[:, e, s : s + take],
                    in_=results[c][:, e, offset : offset + take],
                )

        tiles = [(c, g, t) for c in range(n_chunks) for g in range(HALVES) for t in range(PACK)]

        def tensor_step(index):
            c, g, t = tiles[index]
            first_layer(c, g, t)
            for before in range(n_chunks - 1):
                for half in range(HALVES):
                    if index == HALVES * PACK * (before + 1) + SECOND_LAYER_BEHIND[half]:
                        second_layer(before, (half,))
            if t < PACK - 1:
                return
            if g == 0 and c > 0:
                pool(c)

        def prep_due(c):
            for k in range(len(PREPS)):
                if PREPS[k][0] == c + 2:
                    return k
            return None

        regroup(0)
        sort_w1_tile_scales(0, 0)
        sort_w1_tile_scales(0, 1)
        quantise_patches(0)
        sort_w1_tile_codes(0, 0)
        sort_w1_tile_codes(0, 1)
        for t in range(2, PACK):
            sort_w1_tile_scales(0, t)
            sort_w1_tile_codes(0, t)
        sort_w1_scales(1)
        regroup(1)
        sort_w1_codes(1)
        quantise_patches(1)
        pool(0)
        take_mean(0)
        for index in range(LEAD):
            tensor_step(index)

        for index in range(len(tiles)):
            c, g, t = tiles[index]
            silu(c, g, t)
            if index + LEAD < len(tiles):
                tensor_step(index + LEAD)
            if t < PACK - 1:
                continue
            if g == 0 and c > 0:
                take_mean(c)
            unit = unit_of(c, g)
            if g != unit[1][-1]:
                continue
            last = c == n_chunks - 1
            k = prep_due(c)
            if last:
                if g == 0:
                    interleave(unit)
                    finish(c - 1, 0)
                    continue
                interleave(unit, on_scalar=True)
                for half in range(HALVES):
                    quantise_o2(unit_of(c, half))
                    second_layer(c, (half,))
                finish(c - 1, 1)
                continue
            interleave(unit)
            if c == 0:
                if g == 0:
                    sort_w2_codes()
                else:
                    sort_w2_scales()
            else:
                finish(c - 1, g)
            quantise_o2(unit)
            if k is not None:
                if g == 0:
                    regroup(k)
                else:
                    quantise_patches(k)
        finish(n_chunks - 1, 0)
        finish(n_chunks - 1, 1)
